import numpy as np
import ml_dtypes


def mxq(x, axis, fmt="e4m3"):
    dtype, down = {"e4m3": (ml_dtypes.float8_e4m3fn, 7), "e5m2": (ml_dtypes.float8_e5m2, 14)}[fmt]
    v = np.moveaxis(np.asarray(x, np.float32).astype(ml_dtypes.bfloat16).astype(np.float64), axis, -1)
    blocks = v.reshape(v.shape[:-1] + (-1, 32))
    amax = np.abs(blocks).max(-1, keepdims=True)
    byte = np.maximum(np.where(amax > 0, np.frexp(amax)[1] - 1 + 127, 0) - down, 1)
    scale = np.exp2(byte - 127.0)
    codes = (blocks / scale).astype(np.float32).astype(dtype).astype(np.float64)
    return np.moveaxis((codes * scale).reshape(v.shape), -1, axis)


WIDE = False


def mx_kscale(k):
    if not WIDE:
        return np.ones(k)
    levels = np.array([10, -10, 5, -5, 0])
    a = np.random.permutation(np.resize(levels, k // 512 * 4)).reshape(k // 512, 4)
    idx = np.arange(k)
    return np.exp2(a[idx // 512, idx % 128 // 32])


BF16 = ml_dtypes.bfloat16


def bf(x):
    return np.asarray(x, np.float32).astype(BF16)


def f64(x):
    return np.asarray(x).astype(np.float64)


B, C, T, P, N, D = 8, 16, 2048, 128, 8, 512
L = T // P
G = L // N


def gelu_tanh(v):
    return 0.5 * v * (1.0 + np.tanh(np.sqrt(2.0 / np.pi) * (v + 0.044715 * v**3)))


def setup_inputs():
    s = mx_kscale(D)
    return {'x': bf(np.random.standard_normal((B, C, T))),
            'emb_W': bf(np.random.standard_normal((P, D)) / np.sqrt(P) * s),
            'emb_b': bf(np.random.standard_normal(D) * 0.2 * s),
            'enc_W1': bf(np.random.standard_normal((N, D, D)) / np.sqrt(D) / s[None, :, None]),
            'enc_b1': bf(np.random.standard_normal((N, D)) * 0.2),
            'enc_W2': bf(np.random.standard_normal((N, D, D)) / np.sqrt(D)),
            'enc_b2': bf(np.random.standard_normal((N, D)) * 0.2)}


def reference(x, emb_W, emb_b, enc_W1, enc_b1, enc_W2, enc_b2):
    e = f64(x).reshape(B * C * L, P) @ f64(emb_W) + f64(emb_b)
    e = np.moveaxis(e.reshape(B, C, G, N, D), 3, 0).reshape(N, B * C * G, D)
    a = (mxq(e, 2, 'e4m3') @ mxq(f64(enc_W1), 1, 'e4m3')) + f64(enc_b1)[:, None, :]
    g = gelu_tanh(a)
    o = (mxq(g, 2, 'e4m3') @ mxq(f64(enc_W2), 1, 'e4m3')) + f64(enc_b2)[:, None, :]
    return o.reshape(N, B, C, G, D)

@@ -1,0 +1,239 @@
+from contextlib import ExitStack
+
+import concourse.mybir as mybir
+from concourse.masks import make_identity
+
+BF16 = mybir.dt.bfloat16
+F32 = mybir.dt.float32
+U32 = mybir.dt.uint32
+U8 = mybir.dt.uint8
+FP8X4 = mybir.dt.float8_e4m3fn_x4
+ADD = mybir.AluOpType.add
+GELU = mybir.ActivationFunctionType.Gelu_apprx_tanh
+
+P = 128
+NM = 8
+D = 512
+TOK = 256
+FLOPS = 2 * 2048 * 128 * 512 + 2 * 2 * 2048 * 512 * 512
+
+W_ON_VECTOR = (0, 1, 2)
+
+
+def regroup(copy, dst, src):
+    copy(
+        out=dst.rearrange("p (c i) t -> p c t i", i=4),
+        in_=src.rearrange("p t (c i) -> p c t i", i=4),
+    )
+
+
+def tile_model_pa_kernel(tc, x, emb_W, emb_b, enc_W1, enc_b1, enc_W2, enc_b2, out):
+    nc = tc.nc
+    with ExitStack() as ctx:
+        const = ctx.enter_context(tc.tile_pool(name="const", bufs=1))
+        wraw_pool = ctx.enter_context(tc.tile_pool(name="wraw", bufs=1))
+        wq_pool = ctx.enter_context(tc.tile_pool(name="wq", bufs=1))
+        grp = ctx.enter_context(tc.tile_pool(name="grp", bufs=4))
+        act = ctx.enter_context(tc.tile_pool(name="act", bufs=3))
+        ps_xe = ctx.enter_context(tc.psum_pool(name="ps_xe", bufs=2))
+        ps_a = ctx.enter_context(tc.psum_pool(name="ps_a", bufs=3))
+        ps_o = ctx.enter_context(tc.psum_pool(name="ps_o", bufs=3))
+
+        wraw = []
+        for i in range(2 * NM):
+            wraw.append(wraw_pool.tile([P, 4, D], BF16, name="wraw%d" % i))
+
+        def load_w(i):
+            n = i // 2
+            if i % 2 == 0:
+                src = enc_W1[n].rearrange("(p j) h -> p j h", j=4)
+            else:
+                src = enc_W2[n].rearrange("(t p) d -> p t d", p=P)
+            nc.sync.dma_start(out=wraw[i][:], in_=src)
+
+        x_sb = const.tile([P, 2048], BF16, name="x_sb")
+        embw = const.tile([P, D], BF16, name="embw")
+        eb_bf = const.tile([P, 4], BF16, name="eb_bf")
+        b1rows = const.tile([P, D], BF16, name="b1rows")
+        b2bc = const.tile([P, NM, D], BF16, name="b2bc")
+        warm = const.tile([P, 1], F32, name="warm")
+        warm2 = const.tile([P, 1], F32, name="warm2")
+        ident = const.tile([P, P], BF16, name="ident")
+
+        nc.vector.memset(warm[:], 0.0)
+        nc.vector.memset(b1rows[:], 0.0)
+        make_identity(nc, ident[:])
+
+        load_w(0)
+        nc.sync.dma_start(out=x_sb[:], in_=x.rearrange("b c t -> (b c) t"))
+        nc.sync.dma_start(out=embw[:], in_=emb_W)
+        nc.scalar.dma_start(out=eb_bf[:], in_=emb_b.rearrange("(p t) -> p t", t=4))
+        nc.scalar.dma_start(out=b1rows[0:NM, :], in_=enc_b1)
+        nc.gpsimd.dma_start(
+            out=b2bc[:].rearrange("p n d -> p (n d)"),
+            in_=enc_b2.rearrange("n d -> (n d)").partition_broadcast(P),
+        )
+        for i in range(1, 2 * NM):
+            load_w(i)
+
+        nc.scalar.activation(out=warm2[:], in_=warm[:], func=GELU)
+
+        wc = []
+        ws = []
+        for i in range(2 * NM):
+            wc.append(wq_pool.tile([P, D], U32, name="wc%d" % i, align_bytes=64))
+            ws.append(wq_pool.tile([P, D], U8, name="ws%d" % i, align_bytes=64))
+        wg = {}
+
+        def w_regroup(i):
+            g = grp.tile([P, D, 4], BF16, name="wg", tag="wg", align_bytes=64)
+            wg[i] = g
+            copy = nc.vector.tensor_copy if i in W_ON_VECTOR else nc.scalar.copy
+            regroup(copy, g[:], wraw[i][:])
+
+        def w_quant(i):
+            nc.vector.quantize_mx(
+                out=wc[i][:].bitcast(FP8X4),
+                scales=ws[i][:],
+                in_=wg[i][:].rearrange("p c t -> p (c t)"),
+            )
+
+        embwp = const.tile([P, 4, P], BF16, name="embwp")
+        eb = const.tile([P, 4], F32, name="eb")
+        b1T = const.tile([P, 4, NM], F32, name="b1T")
+        xT = const.tile([P, NM, 2, P], BF16, name="xT")
+
+        def prep_x():
+            for q in range(4):
+                x_ps = ps_xe.tile([P, 4, P], BF16, name="x_ps", tag="xe")
+                for nn in range(2):
+                    for l in range(2):
+                        j = 8 * l + 2 * q + nn
+                        nc.tensor.transpose(x_ps[:, 2 * nn + l, :], x_sb[:, j * P:(j + 1) * P], ident[:])
+                dst = xT[:, 2 * q:2 * q + 2, :, :].rearrange("p n l c -> p (n l) c")
+                if q % 2 == 0:
+                    nc.vector.tensor_copy(out=dst, in_=x_ps[:])
+                else:
+                    nc.scalar.copy(out=dst, in_=x_ps[:])
+
+        def prep_small():
+            nc.vector.tensor_copy(out=embwp[:], in_=embw[:].rearrange("s (m t) -> s t m", t=4))
+            nc.vector.tensor_copy(out=eb[:], in_=eb_bf[:])
+            b_ps = ps_xe.tile([P, 4, P], BF16, name="b_ps", tag="xe")
+            for t in range(4):
+                nc.tensor.transpose(b_ps[:, t, :], b1rows[:, t * P:(t + 1) * P], ident[:])
+            nc.vector.tensor_copy(out=b1T[:], in_=b_ps[:, :, 0:NM])
+
+        ge = {}
+        ec = {}
+        es = {}
+        a_ps = {}
+        gT = {}
+        gg = {}
+        gc = {}
+        gs = {}
+        o_ps = {}
+
+        def emb(n):
+            ge[n] = act.tile([P, TOK, 4], BF16, name="ge", tag="ge", align_bytes=64)
+            for l in range(2):
+                e_ps = ps_xe.tile([P, 4, P], F32, name="e_ps", tag="xe")
+                for t in range(4):
+                    nc.tensor.matmul(e_ps[:, t, :], lhsT=embwp[:, t, :], rhs=xT[:, n, l, :], start=True, stop=True)
+                nc.vector.tensor_tensor(
+                    out=ge[n][:, l * P:(l + 1) * P, :],
+                    in0=e_ps[:].rearrange("p t c -> p c t"),
+                    in1=eb[:].unsqueeze(1).to_broadcast([P, P, 4]),
+                    op=ADD,
+                )
+
+        def e_quant(n):
+            ec[n] = act.tile([P, TOK], U32, name="ec", tag="ec", align_bytes=64)
+            es[n] = act.tile([P, TOK], U8, name="es", tag="es", align_bytes=64)
+            nc.vector.quantize_mx(
+                out=ec[n][:].bitcast(FP8X4),
+                scales=es[n][:],
+                in_=ge[n][:].rearrange("p c t -> p (c t)"),
+            )
+
+        def mx1_gelu(n):
+            gT[n] = act.tile([P, 4, TOK], BF16, name="gT", tag="gT")
+            for h in range(2):
+                a = ps_a.tile([P, 2, TOK], F32, name="a_ps", tag="a")
+                for u in range(2):
+                    t = 2 * h + u
+                    nc.tensor.matmul_mx(
+                        out=a[:, u, :],
+                        lhsT=wc[2 * n][:, t * P:(t + 1) * P].bitcast(FP8X4),
+                        lhsT_scale=ws[2 * n][:, t * P:(t + 1) * P],
+                        rhs=ec[n][:].bitcast(FP8X4),
+                        rhs_scale=es[n][:],
+                        start=True,
+                        stop=True,
+                    )
+                for u in range(2):
+                    t = 2 * h + u
+                    nc.scalar.activation(out=gT[n][:, t, :], in_=a[:, u, :], func=GELU, bias=b1T[:, t, n:n + 1])
+
+        def g_regroup(n):
+            gg[n] = act.tile([P, TOK, 4], BF16, name="gg", tag="gg", align_bytes=64)
+            regroup(nc.vector.tensor_copy, gg[n][:], gT[n][:])
+
+        def g_quant(n):
+            gc[n] = act.tile([P, TOK], U32, name="gc", tag="gc", align_bytes=64)
+            gs[n] = act.tile([P, TOK], U8, name="gs", tag="gs", align_bytes=64)
+            nc.vector.quantize_mx(
+                out=gc[n][:].bitcast(FP8X4),
+                scales=gs[n][:],
+                in_=gg[n][:].rearrange("p c t -> p (c t)"),
+            )
+
+        def mx2(n):
+            o_ps[n] = []
+            for l in range(2):
+                o = ps_o.tile([P, D], F32, name="o_ps", tag="o")
+                o_ps[n].append(o)
+                nc.tensor.matmul_mx(
+                    out=o[:],
+                    lhsT=gc[n][:, l * P:(l + 1) * P].bitcast(FP8X4),
+                    lhsT_scale=gs[n][:, l * P:(l + 1) * P],
+                    rhs=wc[2 * n + 1][:].bitcast(FP8X4),
+                    rhs_scale=ws[2 * n + 1][:],
+                    start=True,
+                    stop=True,
+                )
+
+        def out_store(n):
+            o_sb = act.tile([P, 2, D], F32, name="o_sb", tag="o_sb")
+            for l in range(2):
+                nc.vector.tensor_tensor(out=o_sb[:, l, :], in0=o_ps[n][l][:], in1=b2bc[:, n, :], op=ADD)
+            nc.sync.dma_start(
+                out=out[n].rearrange("b c l d -> (b c) (l d)"),
+                in_=o_sb[:].rearrange("p l d -> p (l d)"),
+            )
+
+        w_regroup(0)
+        prep_small()
+        prep_x()
+        w_regroup(1)
+        emb(0)
+        w_quant(0)
+        e_quant(0)
+        mx1_gelu(0)
+        w_regroup(2)
+        emb(1)
+        w_regroup(3)
+        for n in range(NM):
+            g_regroup(n)
+            w_quant(2 * n + 1)
+            g_quant(n)
+            if n + 1 < NM:
+                e_quant(n + 1)
+                w_quant(2 * n + 2)
+                mx1_gelu(n + 1)
+            mx2(n)
+            if n + 2 < NM:
+                w_regroup(2 * n + 4)
+                emb(n + 2)
+                w_regroup(2 * n + 5)
+            out_store(n)

@@ -17,7 +17,9 @@ D = 512
 TOK = 256
 FLOPS = 2 * 2048 * 128 * 512 + 2 * 2 * 2048 * 512 * 512
 
-W_ON_VECTOR = (0, 1, 2)
+S_COLS_W1 = (0, 128, 256, 384, 384, 384, 384, 384)
+S_COLS_W2 = (0, 512, 512, 512, 512, 512, 384, 256)
+LAG_OUT_FROM = 5
 
 
 def regroup(copy, dst, src):
@@ -35,13 +37,32 @@ def tile_model_pa_kernel(tc, x, emb_W, emb_b, enc_W1, enc_b1, enc_W2, enc_b2, ou
         wq_pool = ctx.enter_context(tc.tile_pool(name="wq", bufs=1))
         grp = ctx.enter_context(tc.tile_pool(name="grp", bufs=4))
         act = ctx.enter_context(tc.tile_pool(name="act", bufs=3))
-        ps_xe = ctx.enter_context(tc.psum_pool(name="ps_xe", bufs=2))
-        ps_a = ctx.enter_context(tc.psum_pool(name="ps_a", bufs=3))
-        ps_o = ctx.enter_context(tc.psum_pool(name="ps_o", bufs=3))
+        psum = ctx.enter_context(tc.psum_pool(name="psum", bufs=1))
+        ctx.enter_context(tc.manual_schedule())
+
+        def valid(n):
+            return 0 <= n < NM
 
         wraw = []
+        wc = []
+        ws = []
         for i in range(2 * NM):
             wraw.append(wraw_pool.tile([P, 4, D], BF16, name="wraw%d" % i))
+            wc.append(wq_pool.tile([P, D], U32, name="wc%d" % i, align_bytes=64))
+            ws.append(wq_pool.tile([P, D], U8, name="ws%d" % i, align_bytes=64))
+        x_sb = const.tile([P, 2, 1024], BF16, name="x_sb")
+        embw = const.tile([P, D], BF16, name="embw")
+        embwp = const.tile([P, 4, P], BF16, name="embwp")
+        eb_bf = const.tile([P, 4], BF16, name="eb_bf")
+        eb = const.tile([P, 4], F32, name="eb")
+        brows = const.tile([P, D], BF16, name="brows")
+        b1T = const.tile([P, 4, NM], F32, name="b1T")
+        b2T = const.tile([P, 4, NM], BF16, name="b2T")
+        b2bc = const.tile([P, NM, D], BF16, name="b2bc")
+        warm = const.tile([P, 1], F32, name="warm")
+        warm2 = const.tile([P, 1], F32, name="warm2")
+        ident = const.tile([P, P], BF16, name="ident")
+        xT = const.tile([P, NM, 2, P], BF16, name="xT")
 
         def load_w(i):
             n = i // 2
@@ -51,45 +72,36 @@ def tile_model_pa_kernel(tc, x, emb_W, emb_b, enc_W1, enc_b1, enc_W2, enc_b2, ou
                 src = enc_W2[n].rearrange("(t p) d -> p t d", p=P)
             nc.sync.dma_start(out=wraw[i][:], in_=src)
 
-        x_sb = const.tile([P, 2048], BF16, name="x_sb")
-        embw = const.tile([P, D], BF16, name="embw")
-        eb_bf = const.tile([P, 4], BF16, name="eb_bf")
-        b1rows = const.tile([P, D], BF16, name="b1rows")
-        b2bc = const.tile([P, NM, D], BF16, name="b2bc")
-        warm = const.tile([P, 1], F32, name="warm")
-        warm2 = const.tile([P, 1], F32, name="warm2")
-        ident = const.tile([P, P], BF16, name="ident")
-
+        nc.vector.memset(brows[:], 0.0)
         nc.vector.memset(warm[:], 0.0)
-        nc.vector.memset(b1rows[:], 0.0)
         make_identity(nc, ident[:])
-
-        load_w(0)
-        nc.sync.dma_start(out=x_sb[:], in_=x.rearrange("b c t -> (b c) t"))
-        nc.sync.dma_start(out=embw[:], in_=emb_W)
+        x_v = x.rearrange("b c (l t) -> (b c) l t", l=2)
         nc.scalar.dma_start(out=eb_bf[:], in_=emb_b.rearrange("(p t) -> p t", t=4))
-        nc.scalar.dma_start(out=b1rows[0:NM, :], in_=enc_b1)
-        nc.gpsimd.dma_start(
-            out=b2bc[:].rearrange("p n d -> p (n d)"),
-            in_=enc_b2.rearrange("n d -> (n d)").partition_broadcast(P),
-        )
-        for i in range(1, 2 * NM):
+        nc.scalar.dma_start(out=brows[0:NM, :], in_=enc_b1)
+        nc.scalar.dma_start(out=brows[NM:2 * NM, :], in_=enc_b2)
+        nc.sync.dma_start(out=embw[:], in_=emb_W)
+        nc.sync.dma_start(out=x_sb[:, :, 0:256], in_=x_v[:, :, 0:256])
+        load_w(0)
+        nc.sync.dma_start(out=x_sb[:, :, 256:1024], in_=x_v[:, :, 256:1024])
+        for i in (2, 4, 1, 6, 3, 8, 5, 10, 7, 12, 9, 14, 11, 13, 15):
             load_w(i)
-
         nc.scalar.activation(out=warm2[:], in_=warm[:], func=GELU)
 
-        wc = []
-        ws = []
-        for i in range(2 * NM):
-            wc.append(wq_pool.tile([P, D], U32, name="wc%d" % i, align_bytes=64))
-            ws.append(wq_pool.tile([P, D], U8, name="ws%d" % i, align_bytes=64))
         wg = {}
 
-        def w_regroup(i):
-            g = grp.tile([P, D, 4], BF16, name="wg", tag="wg", align_bytes=64)
-            wg[i] = g
-            copy = nc.vector.tensor_copy if i in W_ON_VECTOR else nc.scalar.copy
-            regroup(copy, g[:], wraw[i][:])
+        def s_cols(i):
+            return S_COLS_W1[i // 2] if i % 2 == 0 else S_COLS_W2[i // 2]
+
+        def w_regroup_scalar(i):
+            wg[i] = grp.tile([P, D, 4], BF16, name="wg", tag="wg", align_bytes=64)
+            c = s_cols(i)
+            if c > 0:
+                regroup(nc.scalar.copy, wg[i][:, 0:c, :], wraw[i][:, :, 0:c])
+
+        def w_regroup_vector(i):
+            c = s_cols(i)
+            if c < D:
+                regroup(nc.vector.tensor_copy, wg[i][:, c:D, :], wraw[i][:, :, c:D])
 
         def w_quant(i):
             nc.vector.quantize_mx(
@@ -98,36 +110,18 @@ def tile_model_pa_kernel(tc, x, emb_W, emb_b, enc_W1, enc_b1, enc_W2, enc_b2, ou
                 in_=wg[i][:].rearrange("p c t -> p (c t)"),
             )
 
-        embwp = const.tile([P, 4, P], BF16, name="embwp")
-        eb = const.tile([P, 4], F32, name="eb")
-        b1T = const.tile([P, 4, NM], F32, name="b1T")
-        xT = const.tile([P, NM, 2, P], BF16, name="xT")
+        def x_transpose(q, bank, copy):
+            x_ps = psum.tile([P, 4, P], BF16, name="x_ps", tag=bank)
+            for nn in range(2):
+                for l in range(2):
+                    c0 = (2 * q + nn) * P
+                    nc.tensor.transpose(x_ps[:, 2 * nn + l, :], x_sb[:, l, c0:c0 + P], ident[:])
+            copy(out=xT[:, 2 * q:2 * q + 2, :, :].rearrange("p n l c -> p (n l) c"), in_=x_ps[:])
 
-        def prep_x():
-            for q in range(4):
-                x_ps = ps_xe.tile([P, 4, P], BF16, name="x_ps", tag="xe")
-                for nn in range(2):
-                    for l in range(2):
-                        j = 8 * l + 2 * q + nn
-                        nc.tensor.transpose(x_ps[:, 2 * nn + l, :], x_sb[:, j * P:(j + 1) * P], ident[:])
-                dst = xT[:, 2 * q:2 * q + 2, :, :].rearrange("p n l c -> p (n l) c")
-                if q % 2 == 0:
-                    nc.vector.tensor_copy(out=dst, in_=x_ps[:])
-                else:
-                    nc.scalar.copy(out=dst, in_=x_ps[:])
-
-        def prep_small():
-            nc.vector.tensor_copy(out=embwp[:], in_=embw[:].rearrange("s (m t) -> s t m", t=4))
-            nc.vector.tensor_copy(out=eb[:], in_=eb_bf[:])
-            b_ps = ps_xe.tile([P, 4, P], BF16, name="b_ps", tag="xe")
-            for t in range(4):
-                nc.tensor.transpose(b_ps[:, t, :], b1rows[:, t * P:(t + 1) * P], ident[:])
-            nc.vector.tensor_copy(out=b1T[:], in_=b_ps[:, :, 0:NM])
-
+        e_ps = {}
         ge = {}
         ec = {}
         es = {}
-        a_ps = {}
         gT = {}
         gg = {}
         gc = {}
@@ -135,14 +129,19 @@ def tile_model_pa_kernel(tc, x, emb_W, emb_b, enc_W1, enc_b1, enc_W2, enc_b2, ou
         o_ps = {}
 
         def emb(n):
+            for l in range(2):
+                e_ps[(n, l)] = psum.tile([P, 4, P], F32, name="e_ps", tag="e%d" % l)
+                for t in range(4):
+                    nc.tensor.matmul(
+                        e_ps[(n, l)][:, t, :], lhsT=embwp[:, t, :], rhs=xT[:, n, l, :], start=True, stop=True
+                    )
+
+        def e_evac(n):
             ge[n] = act.tile([P, TOK, 4], BF16, name="ge", tag="ge", align_bytes=64)
             for l in range(2):
-                e_ps = ps_xe.tile([P, 4, P], F32, name="e_ps", tag="xe")
-                for t in range(4):
-                    nc.tensor.matmul(e_ps[:, t, :], lhsT=embwp[:, t, :], rhs=xT[:, n, l, :], start=True, stop=True)
                 nc.vector.tensor_tensor(
                     out=ge[n][:, l * P:(l + 1) * P, :],
-                    in0=e_ps[:].rearrange("p t c -> p c t"),
+                    in0=e_ps[(n, l)][:].rearrange("p t c -> p c t"),
                     in1=eb[:].unsqueeze(1).to_broadcast([P, P, 4]),
                     op=ADD,
                 )
@@ -156,10 +155,12 @@ def tile_model_pa_kernel(tc, x, emb_W, emb_b, enc_W1, enc_b1, enc_W2, enc_b2, ou
                 in_=ge[n][:].rearrange("p c t -> p (c t)"),
             )
 
-        def mx1_gelu(n):
-            gT[n] = act.tile([P, 4, TOK], BF16, name="gT", tag="gT")
+        a_ps = {}
+
+        def mx1(n):
             for h in range(2):
-                a = ps_a.tile([P, 2, TOK], F32, name="a_ps", tag="a")
+                a = psum.tile([P, 2, TOK], F32, name="a_ps", tag="a%d" % ((2 * n + h) % 4))
+                a_ps[(n, h)] = a
                 for u in range(2):
                     t = 2 * h + u
                     nc.tensor.matmul_mx(
@@ -171,9 +172,13 @@ def tile_model_pa_kernel(tc, x, emb_W, emb_b, enc_W1, enc_b1, enc_W2, enc_b2, ou
                         start=True,
                         stop=True,
                     )
-                for u in range(2):
-                    t = 2 * h + u
-                    nc.scalar.activation(out=gT[n][:, t, :], in_=a[:, u, :], func=GELU, bias=b1T[:, t, n:n + 1])
+
+        def gelu(n):
+            gT[n] = act.tile([P, 4, TOK], BF16, name="gT", tag="gT")
+            for t in range(4):
+                nc.scalar.activation(
+                    out=gT[n][:, t, :], in_=a_ps[(n, t // 2)][:, t % 2, :], func=GELU, bias=b1T[:, t, n:n + 1]
+                )
 
         def g_regroup(n):
             gg[n] = act.tile([P, TOK, 4], BF16, name="gg", tag="gg", align_bytes=64)
@@ -189,10 +194,10 @@ def tile_model_pa_kernel(tc, x, emb_W, emb_b, enc_W1, enc_b1, enc_W2, enc_b2, ou
             )
 
         def mx2(n):
-            o_ps[n] = []
+            kind = "e" if (n >= LAG_OUT_FROM and n % 2 == 1) else "o"
             for l in range(2):
-                o = ps_o.tile([P, D], F32, name="o_ps", tag="o")
-                o_ps[n].append(o)
+                o = psum.tile([P, D], F32, name="o_ps", tag="%s%d" % (kind, l))
+                o_ps[(n, l)] = o
                 nc.tensor.matmul_mx(
                     out=o[:],
                     lhsT=gc[n][:, l * P:(l + 1) * P].bitcast(FP8X4),
@@ -203,37 +208,72 @@ def tile_model_pa_kernel(tc, x, emb_W, emb_b, enc_W1, enc_b1, enc_W2, enc_b2, ou
                     stop=True,
                 )
 
-        def out_store(n):
+        def out_store(n, split):
             o_sb = act.tile([P, 2, D], F32, name="o_sb", tag="o_sb")
+            dst = out[n].rearrange("b c l d -> (b c) l d")
             for l in range(2):
-                nc.vector.tensor_tensor(out=o_sb[:, l, :], in0=o_ps[n][l][:], in1=b2bc[:, n, :], op=ADD)
-            nc.sync.dma_start(
-                out=out[n].rearrange("b c l d -> (b c) (l d)"),
-                in_=o_sb[:].rearrange("p l d -> p (l d)"),
+                nc.vector.tensor_tensor(out=o_sb[:, l, :], in0=o_ps[(n, l)][:], in1=b2bc[:, n, :], op=ADD)
+                if split:
+                    nc.sync.dma_start(out=dst[:, l, :], in_=o_sb[:, l, :])
+            if not split:
+                nc.sync.dma_start(out=dst, in_=o_sb[:])
+
+        def b2_broadcast(k):
+            bb = psum.tile([P, 2, 4, P], BF16, name="bb_ps", tag="o%d" % (k % 2))
+            for nn in range(2):
+                for t in range(4):
+                    n = 2 * k + nn
+                    nc.tensor.transpose(bb[:, nn, t, :], b2T[:, t, n:n + 1].to_broadcast([P, P]), ident[:])
+            nc.scalar.copy(
+                out=b2bc[:, 2 * k:2 * k + 2, :].rearrange("p n d -> p (n d)"),
+                in_=bb[:].rearrange("p n t c -> p (n t c)"),
             )
 
-        w_regroup(0)
-        prep_small()
-        prep_x()
-        w_regroup(1)
+        nc.vector.tensor_copy(out=embwp[:], in_=embw[:].rearrange("s (m t) -> s t m", t=4))
+        nc.vector.tensor_copy(out=eb[:], in_=eb_bf[:])
+        x_transpose(0, "e0", nc.vector.tensor_copy)
+        bt_ps = psum.tile([P, 4, P], BF16, name="bt_ps", tag="a3")
+        for t in range(4):
+            nc.tensor.transpose(bt_ps[:, t, :], brows[:, t * P:(t + 1) * P], ident[:])
+        nc.vector.tensor_copy(out=b1T[:], in_=bt_ps[:, :, 0:NM])
+        nc.vector.tensor_copy(out=b2T[:], in_=bt_ps[:, :, NM:2 * NM])
         emb(0)
-        w_quant(0)
-        e_quant(0)
-        mx1_gelu(0)
-        w_regroup(2)
-        emb(1)
-        w_regroup(3)
-        for n in range(NM):
-            g_regroup(n)
-            w_quant(2 * n + 1)
-            g_quant(n)
-            if n + 1 < NM:
-                e_quant(n + 1)
-                w_quant(2 * n + 2)
-                mx1_gelu(n + 1)
-            mx2(n)
-            if n + 2 < NM:
-                w_regroup(2 * n + 4)
-                emb(n + 2)
-                w_regroup(2 * n + 5)
-            out_store(n)
+        x_transpose(1, "a0", nc.scalar.copy)
+        x_transpose(2, "a1", nc.scalar.copy)
+        x_transpose(3, "a2", nc.scalar.copy)
+
+        for i in range(-3, NM):
+            mats = []
+            if valid(i + 3):
+                mats.append(2 * (i + 3))
+            if valid(i + 1):
+                mats.append(2 * (i + 1) + 1)
+            if valid(i + 1):
+                gelu(i + 1)
+            for m in mats:
+                w_regroup_scalar(m)
+            if i in (-3, -2):
+                b2_broadcast(2 * (i + 3))
+                b2_broadcast(2 * (i + 3) + 1)
+            for m in mats:
+                w_regroup_vector(m)
+            if valid(i):
+                g_regroup(i)
+                w_quant(2 * i + 1)
+                g_quant(i)
+                mx2(i)
+            if valid(i + 2):
+                e_quant(i + 2)
+                mx1(i + 2)
+            if valid(i + 3):
+                e_evac(i + 3)
+            if valid(i + 4):
+                emb(i + 4)
+            if valid(i + 3):
+                w_quant(2 * (i + 3))
+            if valid(i) and i < LAG_OUT_FROM:
+                out_store(i, False)
+            if i > LAG_OUT_FROM:
+                out_store(i - 1, False)
+            if i == NM - 1:
+                out_store(i, True)

@@ -9,6 +9,7 @@ U32 = mybir.dt.uint32
 U8 = mybir.dt.uint8
 FP8X4 = mybir.dt.float8_e4m3fn_x4
 ADD = mybir.AluOpType.add
+MULT = mybir.AluOpType.mult
 GELU = mybir.ActivationFunctionType.Gelu_apprx_tanh
 
 P = 128
@@ -17,8 +18,10 @@ D = 512
 TOK = 256
 FLOPS = 2 * 2048 * 128 * 512 + 2 * 2 * 2048 * 512 * 512
 
-S_COLS_W1 = (0, 128, 256, 384, 384, 384, 384, 384)
-S_COLS_W2 = (0, 512, 512, 512, 512, 512, 384, 256)
+S_COLS_W1 = (0, 128, 256, 384, 256, 256, 256, 256)
+S_COLS_W2 = (64, 512, 512, 512, 512, 512, 256, 256)
+G_COLS = {4: 128, 6: 128, 8: 256, 10: 256, 12: 256, 14: 256, 13: 256}
+G_STEP = {-2: 4, -1: 6, 0: 8, 1: 10, 2: 12, 3: 14, 4: 13}
 LAG_OUT_FROM = 5
 
 
@@ -100,15 +103,44 @@ def tile_model_pa_kernel(tc, x, emb_W, emb_b, enc_W1, enc_b1, enc_W2, enc_b2, ou
 
         def w_regroup_vector(i):
             c = s_cols(i)
-            if c < D:
-                regroup(nc.vector.tensor_copy, wg[i][:, c:D, :], wraw[i][:, :, c:D])
+            end = D - G_COLS.get(i, 0)
+            if c < end:
+                regroup(nc.vector.tensor_copy, wg[i][:, c:end, :], wraw[i][:, :, c:end])
+
+        def quant_cols(i, src, c0, width):
+            nc.vector.quantize_mx(
+                out=wc[i][:, c0:c0 + width].bitcast(FP8X4),
+                scales=ws[i][:, c0:c0 + width],
+                in_=src.rearrange("p c t -> p (c t)"),
+            )
 
         def w_quant(i):
-            nc.vector.quantize_mx(
-                out=wc[i][:].bitcast(FP8X4),
-                scales=ws[i][:],
-                in_=wg[i][:].rearrange("p c t -> p (c t)"),
+            end = D - G_COLS.get(i, 0)
+            c0 = 0
+            for width in (512, 256, 128):
+                if end - c0 >= width:
+                    quant_cols(i, wg[i][:, c0:c0 + width, :], c0, width)
+                    c0 += width
+
+        wgg = {}
+
+        def g_piece(i, first):
+            width = G_COLS[i]
+            wgg[i] = grp.tile([P, 256, 4], BF16, name="wgg", tag="wgg", bufs=1, align_bytes=64)
+            if first:
+                nc.vector.memset(wgg[i][:, 0:8, :], 0.0)
+            nc.gpsimd.tensor_scalar(
+                out=wgg[i][:, 0:width, :],
+                in0=wraw[i][:, :, D - width:D].rearrange("p t c -> p c t"),
+                scalar1=1.0,
+                scalar2=0.0,
+                op0=MULT,
+                op1=ADD,
             )
+
+        def g_piece_quant(i):
+            width = G_COLS[i]
+            quant_cols(i, wgg[i][:, 0:width, :], D - width, width)
 
         def x_transpose(q, bank, copy):
             x_ps = psum.tile([P, 4, P], BF16, name="x_ps", tag=bank)
@@ -266,11 +298,15 @@ def tile_model_pa_kernel(tc, x, emb_W, emb_b, enc_W1, enc_b1, enc_W2, enc_b2, ou
                 e_quant(i + 2)
                 mx1(i + 2)
             if valid(i + 3):
+                w_quant(2 * (i + 3))
+            if (i - 1) in G_STEP:
+                g_piece_quant(G_STEP[i - 1])
+            if i in G_STEP:
+                g_piece(G_STEP[i], i == -2)
+            if valid(i + 3):
                 e_evac(i + 3)
             if valid(i + 4):
                 emb(i + 4)
-            if valid(i + 3):
-                w_quant(2 * (i + 3))
             if valid(i) and i < LAG_OUT_FROM:
                 out_store(i, False)
             if i > LAG_OUT_FROM:

@@ -18,8 +18,9 @@ D = 512
 TOK = 256
 FLOPS = 2 * 2048 * 128 * 512 + 2 * 2 * 2048 * 512 * 512
 
-S_COLS_W1 = (0, 128, 256, 384, 256, 256, 256, 256)
-S_COLS_W2 = (64, 512, 512, 512, 512, 512, 256, 256)
+S_COLS_W1 = (192, 128, 128, 320, 256, 256, 256, 256)
+S_COLS_W2 = (0, 512, 512, 512, 512, 512, 256, 0)
+G_ON_SCALAR = (6, 7)
 G_COLS = {4: 128, 6: 128, 8: 256, 10: 256, 12: 256, 14: 256, 13: 256}
 G_STEP = {-2: 4, -1: 6, 0: 8, 1: 10, 2: 12, 3: 14, 4: 13}
 LAG_OUT_FROM = 5
@@ -212,9 +213,9 @@ def tile_model_pa_kernel(tc, x, emb_W, emb_b, enc_W1, enc_b1, enc_W2, enc_b2, ou
                     out=gT[n][:, t, :], in_=a_ps[(n, t // 2)][:, t % 2, :], func=GELU, bias=b1T[:, t, n:n + 1]
                 )
 
-        def g_regroup(n):
+        def g_regroup(n, copy):
             gg[n] = act.tile([P, TOK, 4], BF16, name="gg", tag="gg", align_bytes=64)
-            regroup(nc.vector.tensor_copy, gg[n][:], gT[n][:])
+            regroup(copy, gg[n][:], gT[n][:])
 
         def g_quant(n):
             gc[n] = act.tile([P, TOK], U32, name="gc", tag="gc", align_bytes=64)
@@ -270,6 +271,7 @@ def tile_model_pa_kernel(tc, x, emb_W, emb_b, enc_W1, enc_b1, enc_W2, enc_b2, ou
         nc.vector.tensor_copy(out=b1T[:], in_=bt_ps[:, :, 0:NM])
         nc.vector.tensor_copy(out=b2T[:], in_=bt_ps[:, :, NM:2 * NM])
         emb(0)
+        w_regroup_scalar(0)
         x_transpose(1, "a0", nc.scalar.copy)
         x_transpose(2, "a1", nc.scalar.copy)
         x_transpose(3, "a2", nc.scalar.copy)
@@ -282,15 +284,19 @@ def tile_model_pa_kernel(tc, x, emb_W, emb_b, enc_W1, enc_b1, enc_W2, enc_b2, ou
                 mats.append(2 * (i + 1) + 1)
             if valid(i + 1):
                 gelu(i + 1)
+                if (i + 1) in G_ON_SCALAR:
+                    g_regroup(i + 1, nc.scalar.copy)
             for m in mats:
-                w_regroup_scalar(m)
-            if i in (-3, -2):
-                b2_broadcast(2 * (i + 3))
-                b2_broadcast(2 * (i + 3) + 1)
+                if m > 0:
+                    w_regroup_scalar(m)
+            if i in (-2, -1):
+                b2_broadcast(2 * (i + 2))
+                b2_broadcast(2 * (i + 2) + 1)
             for m in mats:
                 w_regroup_vector(m)
             if valid(i):
-                g_regroup(i)
+                if i not in G_ON_SCALAR:
+                    g_regroup(i, nc.vector.tensor_copy)
                 w_quant(2 * i + 1)
                 g_quant(i)
                 mx2(i)

@@ -42,7 +42,6 @@ def tile_model_pa_kernel(tc, x, emb_W, emb_b, enc_W1, enc_b1, enc_W2, enc_b2, ou
         grp = ctx.enter_context(tc.tile_pool(name="grp", bufs=4))
         act = ctx.enter_context(tc.tile_pool(name="act", bufs=3))
         psum = ctx.enter_context(tc.psum_pool(name="psum", bufs=1))
-        ctx.enter_context(tc.manual_schedule())
 
         def valid(n):
             return 0 <= n < NM

@@ -42,6 +42,7 @@ def tile_model_pa_kernel(tc, x, emb_W, emb_b, enc_W1, enc_b1, enc_W2, enc_b2, ou
         grp = ctx.enter_context(tc.tile_pool(name="grp", bufs=4))
         act = ctx.enter_context(tc.tile_pool(name="act", bufs=3))
         psum = ctx.enter_context(tc.psum_pool(name="psum", bufs=1))
+        ctx.enter_context(tc.manual_schedule())
 
         def valid(n):
             return 0 <= n < NM
@@ -291,6 +292,9 @@ def tile_model_pa_kernel(tc, x, emb_W, emb_b, enc_W1, enc_b1, enc_W2, enc_b2, ou
             if i in (-2, -1):
                 b2_broadcast(2 * (i + 2))
                 b2_broadcast(2 * (i + 2) + 1)
+            if valid(i + 2):
+                e_quant(i + 2)
+                mx1(i + 2)
             for m in mats:
                 w_regroup_vector(m)
             if valid(i):
@@ -299,9 +303,6 @@ def tile_model_pa_kernel(tc, x, emb_W, emb_b, enc_W1, enc_b1, enc_W2, enc_b2, ou
                 w_quant(2 * i + 1)
                 g_quant(i)
                 mx2(i)
-            if valid(i + 2):
-                e_quant(i + 2)
-                mx1(i + 2)
             if valid(i + 3):
                 w_quant(2 * (i + 3))
             if (i - 1) in G_STEP:

@@ -19,7 +19,7 @@ TOK = 256
 FLOPS = 2 * 2048 * 128 * 512 + 2 * 2 * 2048 * 512 * 512
 
 S_COLS_W1 = (192, 128, 128, 320, 256, 256, 256, 256)
-S_COLS_W2 = (0, 512, 512, 512, 512, 512, 256, 0)
+S_COLS_W2 = (0, 448, 448, 448, 448, 448, 256, 0)
 G_ON_SCALAR = (6, 7)
 G_COLS = {4: 128, 6: 128, 8: 256, 10: 256, 12: 256, 14: 256, 13: 256}
 G_STEP = {-2: 4, -1: 6, 0: 8, 1: 10, 2: 12, 3: 14, 4: 13}

@@ -13,23 +13,27 @@ MULT = mybir.AluOpType.mult
 GELU = mybir.ActivationFunctionType.Gelu_apprx_tanh
 
 P = 128
-NM = 8
+PACK = 4
+MODELS = 8
 D = 512
-TOK = 256
+TOKENS = 256
 FLOPS = 2 * 2048 * 128 * 512 + 2 * 2 * 2048 * 512 * 512
 
-S_COLS_W1 = (192, 128, 128, 320, 256, 256, 256, 256)
-S_COLS_W2 = (0, 448, 448, 448, 448, 448, 256, 0)
-G_ON_SCALAR = (6, 7)
-G_COLS = {4: 128, 6: 128, 8: 256, 10: 256, 12: 256, 14: 256, 13: 256}
-G_STEP = {-2: 4, -1: 6, 0: 8, 1: 10, 2: 12, 3: 14, 4: 13}
-LAG_OUT_FROM = 5
+W1_SPLIT = D // 2
+GPSIMD_LEAD = 4
+GPSIMD_FROM = 4
+LATE_OUTPUT_FROM = MODELS - 3
+SCALAR_REGROUPS_G_FROM = MODELS - 2
+FIRST_STEP = -3
+X_HALF = 1024
+FIRST_X_COLS = 2 * P
+HOLD_COLS = 8
 
 
-def regroup(copy, dst, src):
+def regroup(copy, grouped, planes):
     copy(
-        out=dst.rearrange("p (c i) t -> p c t i", i=4),
-        in_=src.rearrange("p t (c i) -> p c t i", i=4),
+        out=grouped.rearrange("p (c r) t -> p c t r", r=4),
+        in_=planes.rearrange("p t (c r) -> p c t r", r=4),
     )
 
 
@@ -44,34 +48,42 @@ def tile_model_pa_kernel(tc, x, emb_W, emb_b, enc_W1, enc_b1, enc_W2, enc_b2, ou
         psum = ctx.enter_context(tc.psum_pool(name="psum", bufs=1))
         ctx.enter_context(tc.manual_schedule())
 
-        def valid(n):
-            return 0 <= n < NM
+        def is_model(n):
+            return 0 <= n < MODELS
+
+        def matrices_of(step):
+            matrices = []
+            if is_model(step + 3):
+                matrices.append(2 * (step + 3))
+            if is_model(step + 1):
+                matrices.append(2 * (step + 1) + 1)
+            return matrices
 
         wraw = []
         wc = []
         ws = []
-        for i in range(2 * NM):
-            wraw.append(wraw_pool.tile([P, 4, D], BF16, name="wraw%d" % i))
+        for i in range(2 * MODELS):
+            wraw.append(wraw_pool.tile([P, PACK, D], BF16, name="wraw%d" % i))
             wc.append(wq_pool.tile([P, D], U32, name="wc%d" % i, align_bytes=64))
             ws.append(wq_pool.tile([P, D], U8, name="ws%d" % i, align_bytes=64))
-        x_sb = const.tile([P, 2, 1024], BF16, name="x_sb")
+        x_sb = const.tile([P, 2, X_HALF], BF16, name="x_sb")
         embw = const.tile([P, D], BF16, name="embw")
-        embwp = const.tile([P, 4, P], BF16, name="embwp")
-        eb_bf = const.tile([P, 4], BF16, name="eb_bf")
-        eb = const.tile([P, 4], F32, name="eb")
+        embwp = const.tile([P, PACK, P], BF16, name="embwp")
+        eb_bf = const.tile([P, PACK], BF16, name="eb_bf")
+        eb = const.tile([P, PACK], F32, name="eb")
         brows = const.tile([P, D], BF16, name="brows")
-        b1T = const.tile([P, 4, NM], F32, name="b1T")
-        b2T = const.tile([P, 4, NM], BF16, name="b2T")
-        b2bc = const.tile([P, NM, D], BF16, name="b2bc")
+        b1T = const.tile([P, PACK, MODELS], F32, name="b1T")
+        b2T = const.tile([P, PACK, MODELS], BF16, name="b2T")
+        b2bc = const.tile([P, MODELS, D], BF16, name="b2bc")
         warm = const.tile([P, 1], F32, name="warm")
         warm2 = const.tile([P, 1], F32, name="warm2")
         ident = const.tile([P, P], BF16, name="ident")
-        xT = const.tile([P, NM, 2, P], BF16, name="xT")
+        xT = const.tile([P, MODELS, 2, P], BF16, name="xT")
 
-        def load_w(i):
+        def load_weights(i):
             n = i // 2
             if i % 2 == 0:
-                src = enc_W1[n].rearrange("(p j) h -> p j h", j=4)
+                src = enc_W1[n].rearrange("(p t) h -> p t h", t=PACK)
             else:
                 src = enc_W2[n].rearrange("(t p) d -> p t d", p=P)
             nc.sync.dma_start(out=wraw[i][:], in_=src)
@@ -79,125 +91,126 @@ def tile_model_pa_kernel(tc, x, emb_W, emb_b, enc_W1, enc_b1, enc_W2, enc_b2, ou
         nc.vector.memset(brows[:], 0.0)
         nc.vector.memset(warm[:], 0.0)
         make_identity(nc, ident[:])
-        x_v = x.rearrange("b c (l t) -> (b c) l t", l=2)
-        nc.scalar.dma_start(out=eb_bf[:], in_=emb_b.rearrange("(p t) -> p t", t=4))
-        nc.scalar.dma_start(out=brows[0:NM, :], in_=enc_b1)
-        nc.scalar.dma_start(out=brows[NM:2 * NM, :], in_=enc_b2)
+        x_v = x.rearrange("b c (l y) -> (b c) l y", l=2)
+        nc.scalar.dma_start(out=eb_bf[:], in_=emb_b.rearrange("(p t) -> p t", t=PACK))
+        nc.scalar.dma_start(out=brows[0:MODELS, :], in_=enc_b1)
+        nc.scalar.dma_start(out=brows[MODELS:2 * MODELS, :], in_=enc_b2)
         nc.sync.dma_start(out=embw[:], in_=emb_W)
-        nc.sync.dma_start(out=x_sb[:, :, 0:256], in_=x_v[:, :, 0:256])
-        load_w(0)
-        nc.sync.dma_start(out=x_sb[:, :, 256:1024], in_=x_v[:, :, 256:1024])
-        for i in (2, 4, 1, 6, 3, 8, 5, 10, 7, 12, 9, 14, 11, 13, 15):
-            load_w(i)
+        nc.sync.dma_start(out=x_sb[:, :, 0:FIRST_X_COLS], in_=x_v[:, :, 0:FIRST_X_COLS])
+        load_order = []
+        for step in range(FIRST_STEP, MODELS):
+            load_order.extend(matrices_of(step))
+        load_weights(load_order[0])
+        nc.sync.dma_start(out=x_sb[:, :, FIRST_X_COLS:X_HALF], in_=x_v[:, :, FIRST_X_COLS:X_HALF])
+        for i in load_order[1:]:
+            load_weights(i)
         nc.scalar.activation(out=warm2[:], in_=warm[:], func=GELU)
 
         wg = {}
+        wgg = {}
 
-        def s_cols(i):
-            return S_COLS_W1[i // 2] if i % 2 == 0 else S_COLS_W2[i // 2]
+        def shares(i):
+            n = i // 2
+            if i % 2 == 0:
+                return (W1_SPLIT, D if n < GPSIMD_FROM else W1_SPLIT)
+            if n == 0 or n == MODELS - 1:
+                return (0, D)
+            return (D, D)
 
         def w_regroup_scalar(i):
-            wg[i] = grp.tile([P, D, 4], BF16, name="wg", tag="wg", align_bytes=64)
-            c = s_cols(i)
-            if c > 0:
-                regroup(nc.scalar.copy, wg[i][:, 0:c, :], wraw[i][:, :, 0:c])
+            wg[i] = grp.tile([P, D, PACK], BF16, name="wg", tag="wg", align_bytes=64)
+            s_end = shares(i)[0]
+            if s_end > 0:
+                regroup(nc.scalar.copy, wg[i][:, 0:s_end, :], wraw[i][:, :, 0:s_end])
 
         def w_regroup_vector(i):
-            c = s_cols(i)
-            end = D - G_COLS.get(i, 0)
-            if c < end:
-                regroup(nc.vector.tensor_copy, wg[i][:, c:end, :], wraw[i][:, :, c:end])
+            s_end, v_end = shares(i)
+            if s_end < v_end:
+                regroup(nc.vector.tensor_copy, wg[i][:, s_end:v_end, :], wraw[i][:, :, s_end:v_end])
 
-        def quant_cols(i, src, c0, width):
+        def quantise_cols(i, grouped, c0, width):
             nc.vector.quantize_mx(
                 out=wc[i][:, c0:c0 + width].bitcast(FP8X4),
                 scales=ws[i][:, c0:c0 + width],
-                in_=src.rearrange("p c t -> p (c t)"),
+                in_=grouped.rearrange("p c t -> p (c t)"),
             )
 
-        def w_quant(i):
-            end = D - G_COLS.get(i, 0)
-            c0 = 0
-            for width in (512, 256, 128):
-                if end - c0 >= width:
-                    quant_cols(i, wg[i][:, c0:c0 + width, :], c0, width)
-                    c0 += width
+        def w_quantise(i):
+            v_end = shares(i)[1]
+            quantise_cols(i, wg[i][:, 0:v_end, :], 0, v_end)
 
-        wgg = {}
-
-        def g_piece(i, first):
-            width = G_COLS[i]
-            wgg[i] = grp.tile([P, 256, 4], BF16, name="wgg", tag="wgg", bufs=1, align_bytes=64)
+        def w_regroup_gpsimd(i, first):
+            v_end = shares(i)[1]
+            wgg[i] = grp.tile([P, D - W1_SPLIT, PACK], BF16, name="wgg", tag="wgg", bufs=1, align_bytes=64)
             if first:
-                nc.vector.memset(wgg[i][:, 0:8, :], 0.0)
+                nc.vector.memset(wgg[i][:, 0:HOLD_COLS, :], 0.0)
             nc.gpsimd.tensor_scalar(
-                out=wgg[i][:, 0:width, :],
-                in0=wraw[i][:, :, D - width:D].rearrange("p t c -> p c t"),
+                out=wgg[i][:],
+                in0=wraw[i][:, :, v_end:D].rearrange("p t c -> p c t"),
                 scalar1=1.0,
                 scalar2=0.0,
                 op0=MULT,
                 op1=ADD,
             )
 
-        def g_piece_quant(i):
-            width = G_COLS[i]
-            quant_cols(i, wgg[i][:, 0:width, :], D - width, width)
+        def w_quantise_gpsimd(i):
+            v_end = shares(i)[1]
+            quantise_cols(i, wgg[i][:], v_end, D - v_end)
 
-        def x_transpose(q, bank, copy):
+        def x_transpose(pair, bank, copy):
             x_ps = psum.tile([P, 4, P], BF16, name="x_ps", tag=bank)
             for nn in range(2):
                 for l in range(2):
-                    c0 = (2 * q + nn) * P
+                    c0 = (2 * pair + nn) * P
                     nc.tensor.transpose(x_ps[:, 2 * nn + l, :], x_sb[:, l, c0:c0 + P], ident[:])
-            copy(out=xT[:, 2 * q:2 * q + 2, :, :].rearrange("p n l c -> p (n l) c"), in_=x_ps[:])
+            copy(out=xT[:, 2 * pair:2 * pair + 2, :, :].rearrange("p n l c -> p (n l) c"), in_=x_ps[:])
 
         e_ps = {}
         ge = {}
         ec = {}
         es = {}
+        a_ps = {}
         gT = {}
         gg = {}
         gc = {}
         gs = {}
         o_ps = {}
 
-        def emb(n):
+        def embed(n):
             for l in range(2):
-                e_ps[(n, l)] = psum.tile([P, 4, P], F32, name="e_ps", tag="e%d" % l)
-                for t in range(4):
+                e_ps[(n, l)] = psum.tile([P, PACK, P], F32, name="e_ps", tag="e%d" % l)
+                for t in range(PACK):
                     nc.tensor.matmul(
                         e_ps[(n, l)][:, t, :], lhsT=embwp[:, t, :], rhs=xT[:, n, l, :], start=True, stop=True
                     )
 
-        def e_evac(n):
-            ge[n] = act.tile([P, TOK, 4], BF16, name="ge", tag="ge", align_bytes=64)
+        def e_out_of_psum(n):
+            ge[n] = act.tile([P, TOKENS, PACK], BF16, name="ge", tag="ge", align_bytes=64)
             for l in range(2):
                 nc.vector.tensor_tensor(
                     out=ge[n][:, l * P:(l + 1) * P, :],
                     in0=e_ps[(n, l)][:].rearrange("p t c -> p c t"),
-                    in1=eb[:].unsqueeze(1).to_broadcast([P, P, 4]),
+                    in1=eb[:].unsqueeze(1).to_broadcast([P, P, PACK]),
                     op=ADD,
                 )
 
-        def e_quant(n):
-            ec[n] = act.tile([P, TOK], U32, name="ec", tag="ec", align_bytes=64)
-            es[n] = act.tile([P, TOK], U8, name="es", tag="es", align_bytes=64)
+        def e_quantise(n):
+            ec[n] = act.tile([P, TOKENS], U32, name="ec", tag="ec", align_bytes=64)
+            es[n] = act.tile([P, TOKENS], U8, name="es", tag="es", align_bytes=64)
             nc.vector.quantize_mx(
                 out=ec[n][:].bitcast(FP8X4),
                 scales=es[n][:],
                 in_=ge[n][:].rearrange("p c t -> p (c t)"),
             )
 
-        a_ps = {}
-
-        def mx1(n):
-            for h in range(2):
-                a = psum.tile([P, 2, TOK], F32, name="a_ps", tag="a%d" % ((2 * n + h) % 4))
-                a_ps[(n, h)] = a
-                for u in range(2):
-                    t = 2 * h + u
+        def layer1(n):
+            for t_hi in range(2):
+                a = psum.tile([P, 2, TOKENS], F32, name="a_ps", tag="a%d" % ((2 * n + t_hi) % 4))
+                a_ps[(n, t_hi)] = a
+                for t_lo in range(2):
+                    t = 2 * t_hi + t_lo
                     nc.tensor.matmul_mx(
-                        out=a[:, u, :],
+                        out=a[:, t_lo, :],
                         lhsT=wc[2 * n][:, t * P:(t + 1) * P].bitcast(FP8X4),
                         lhsT_scale=ws[2 * n][:, t * P:(t + 1) * P],
                         rhs=ec[n][:].bitcast(FP8X4),
@@ -207,27 +220,27 @@ def tile_model_pa_kernel(tc, x, emb_W, emb_b, enc_W1, enc_b1, enc_W2, enc_b2, ou
                     )
 
         def gelu(n):
-            gT[n] = act.tile([P, 4, TOK], BF16, name="gT", tag="gT")
-            for t in range(4):
+            gT[n] = act.tile([P, PACK, TOKENS], BF16, name="gT", tag="gT")
+            for t in range(PACK):
                 nc.scalar.activation(
                     out=gT[n][:, t, :], in_=a_ps[(n, t // 2)][:, t % 2, :], func=GELU, bias=b1T[:, t, n:n + 1]
                 )
 
         def g_regroup(n, copy):
-            gg[n] = act.tile([P, TOK, 4], BF16, name="gg", tag="gg", align_bytes=64)
+            gg[n] = act.tile([P, TOKENS, PACK], BF16, name="gg", tag="gg", align_bytes=64)
             regroup(copy, gg[n][:], gT[n][:])
 
-        def g_quant(n):
-            gc[n] = act.tile([P, TOK], U32, name="gc", tag="gc", align_bytes=64)
-            gs[n] = act.tile([P, TOK], U8, name="gs", tag="gs", align_bytes=64)
+        def g_quantise(n):
+            gc[n] = act.tile([P, TOKENS], U32, name="gc", tag="gc", align_bytes=64)
+            gs[n] = act.tile([P, TOKENS], U8, name="gs", tag="gs", align_bytes=64)
             nc.vector.quantize_mx(
                 out=gc[n][:].bitcast(FP8X4),
                 scales=gs[n][:],
                 in_=gg[n][:].rearrange("p c t -> p (c t)"),
             )
 
-        def mx2(n):
-            kind = "e" if (n >= LAG_OUT_FROM and n % 2 == 1) else "o"
+        def layer2(n):
+            kind = "e" if (n >= LATE_OUTPUT_FROM and n % 2 == 1) else "o"
             for l in range(2):
                 o = psum.tile([P, D], F32, name="o_ps", tag="%s%d" % (kind, l))
                 o_ps[(n, l)] = o
@@ -241,81 +254,78 @@ def tile_model_pa_kernel(tc, x, emb_W, emb_b, enc_W1, enc_b1, enc_W2, enc_b2, ou
                     stop=True,
                 )
 
-        def out_store(n, split):
+        def output(n, store_each_bank):
             o_sb = act.tile([P, 2, D], F32, name="o_sb", tag="o_sb")
             dst = out[n].rearrange("b c l d -> (b c) l d")
             for l in range(2):
                 nc.vector.tensor_tensor(out=o_sb[:, l, :], in0=o_ps[(n, l)][:], in1=b2bc[:, n, :], op=ADD)
-                if split:
+                if store_each_bank:
                     nc.sync.dma_start(out=dst[:, l, :], in_=o_sb[:, l, :])
-            if not split:
+            if not store_each_bank:
                 nc.sync.dma_start(out=dst, in_=o_sb[:])
 
-        def b2_broadcast(k):
-            bb = psum.tile([P, 2, 4, P], BF16, name="bb_ps", tag="o%d" % (k % 2))
+        def spread_b2(pair):
+            bb = psum.tile([P, 2, PACK, P], BF16, name="bb_ps", tag="o%d" % (pair % 2))
             for nn in range(2):
-                for t in range(4):
-                    n = 2 * k + nn
+                for t in range(PACK):
+                    n = 2 * pair + nn
                     nc.tensor.transpose(bb[:, nn, t, :], b2T[:, t, n:n + 1].to_broadcast([P, P]), ident[:])
             nc.scalar.copy(
-                out=b2bc[:, 2 * k:2 * k + 2, :].rearrange("p n d -> p (n d)"),
+                out=b2bc[:, 2 * pair:2 * pair + 2, :].rearrange("p n d -> p (n d)"),
                 in_=bb[:].rearrange("p n t c -> p (n t c)"),
             )
 
-        nc.vector.tensor_copy(out=embwp[:], in_=embw[:].rearrange("s (m t) -> s t m", t=4))
+        nc.vector.tensor_copy(out=embwp[:], in_=embw[:].rearrange("p (m t) -> p t m", t=PACK))
         nc.vector.tensor_copy(out=eb[:], in_=eb_bf[:])
         x_transpose(0, "e0", nc.vector.tensor_copy)
-        bt_ps = psum.tile([P, 4, P], BF16, name="bt_ps", tag="a3")
-        for t in range(4):
+        bt_ps = psum.tile([P, PACK, P], BF16, name="bt_ps", tag="a3")
+        for t in range(PACK):
             nc.tensor.transpose(bt_ps[:, t, :], brows[:, t * P:(t + 1) * P], ident[:])
-        nc.vector.tensor_copy(out=b1T[:], in_=bt_ps[:, :, 0:NM])
-        nc.vector.tensor_copy(out=b2T[:], in_=bt_ps[:, :, NM:2 * NM])
-        emb(0)
+        nc.vector.tensor_copy(out=b1T[:], in_=bt_ps[:, :, 0:MODELS])
+        nc.vector.tensor_copy(out=b2T[:], in_=bt_ps[:, :, MODELS:2 * MODELS])
+        embed(0)
         w_regroup_scalar(0)
         x_transpose(1, "a0", nc.scalar.copy)
         x_transpose(2, "a1", nc.scalar.copy)
         x_transpose(3, "a2", nc.scalar.copy)
 
-        for i in range(-3, NM):
-            mats = []
-            if valid(i + 3):
-                mats.append(2 * (i + 3))
-            if valid(i + 1):
-                mats.append(2 * (i + 1) + 1)
-            if valid(i + 1):
-                gelu(i + 1)
-                if (i + 1) in G_ON_SCALAR:
-                    g_regroup(i + 1, nc.scalar.copy)
-            for m in mats:
-                if m > 0:
-                    w_regroup_scalar(m)
-            if i in (-2, -1):
-                b2_broadcast(2 * (i + 2))
-                b2_broadcast(2 * (i + 2) + 1)
-            if valid(i + 2):
-                e_quant(i + 2)
-                mx1(i + 2)
-            for m in mats:
-                w_regroup_vector(m)
-            if valid(i):
-                if i not in G_ON_SCALAR:
-                    g_regroup(i, nc.vector.tensor_copy)
-                w_quant(2 * i + 1)
-                g_quant(i)
-                mx2(i)
-            if valid(i + 3):
-                w_quant(2 * (i + 3))
-            if (i - 1) in G_STEP:
-                g_piece_quant(G_STEP[i - 1])
-            if i in G_STEP:
-                g_piece(G_STEP[i], i == -2)
-            if valid(i + 3):
-                e_evac(i + 3)
-            if valid(i + 4):
-                emb(i + 4)
-            if valid(i) and i < LAG_OUT_FROM:
-                out_store(i, False)
-            if i > LAG_OUT_FROM:
-                out_store(i - 1, False)
-            if i == NM - 1:
-                out_store(i, True)
+        for step in range(FIRST_STEP, MODELS):
+            matrices = matrices_of(step)
+            if is_model(step + 1):
+                gelu(step + 1)
+                if step + 1 >= SCALAR_REGROUPS_G_FROM:
+                    g_regroup(step + 1, nc.scalar.copy)
+            for i in matrices:
+                if i > 0:
+                    w_regroup_scalar(i)
+            if step in (-2, -1):
+                spread_b2(2 * (step + 2))
+                spread_b2(2 * (step + 2) + 1)
+            if is_model(step + 2):
+                e_quantise(step + 2)
+                layer1(step + 2)
+            for i in matrices:
+                w_regroup_vector(i)
+            if is_model(step):
+                if step < SCALAR_REGROUPS_G_FROM:
+                    g_regroup(step, nc.vector.tensor_copy)
+                w_quantise(2 * step + 1)
+                g_quantise(step)
+                layer2(step)
+            if is_model(step + 3):
+                w_quantise(2 * (step + 3))
+                if step + 3 >= GPSIMD_FROM:
+                    w_quantise_gpsimd(2 * (step + 3))
+            ahead = step + GPSIMD_LEAD
+            if is_model(ahead) and ahead >= GPSIMD_FROM:
+                w_regroup_gpsimd(2 * ahead, ahead == GPSIMD_FROM)
+            if is_model(step + 3):
+                e_out_of_psum(step + 3)
+            if is_model(step + 4):
+                embed(step + 4)
+            if is_model(step) and step < LATE_OUTPUT_FROM:
+                output(step, False)
+            if step > LATE_OUTPUT_FROM:
+                output(step - 1, False)
+            if step == MODELS - 1:
+                output(step, True)

@@ -19,15 +19,13 @@ D = 512
 TOKENS = 256
 FLOPS = 2 * 2048 * 128 * 512 + 2 * 2 * 2048 * 512 * 512
 
-W1_SPLIT = D // 2
-GPSIMD_LEAD = 4
-GPSIMD_FROM = 4
-LATE_OUTPUT_FROM = MODELS - 3
+HALF = D // 2
+GPSIMD_EARLY = 4
+LATE_OUTPUT_FROM = MODELS - 2
 SCALAR_REGROUPS_G_FROM = MODELS - 2
-FIRST_STEP = -3
+E_FIRST = 4
 X_HALF = 1024
 FIRST_X_COLS = 2 * P
-HOLD_COLS = 8
 
 
 def regroup(copy, grouped, planes):
@@ -43,21 +41,13 @@ def tile_model_pa_kernel(tc, x, emb_W, emb_b, enc_W1, enc_b1, enc_W2, enc_b2, ou
         const = ctx.enter_context(tc.tile_pool(name="const", bufs=1))
         wraw_pool = ctx.enter_context(tc.tile_pool(name="wraw", bufs=1))
         wq_pool = ctx.enter_context(tc.tile_pool(name="wq", bufs=1))
-        grp = ctx.enter_context(tc.tile_pool(name="grp", bufs=4))
+        grp = ctx.enter_context(tc.tile_pool(name="grp", bufs=5))
         act = ctx.enter_context(tc.tile_pool(name="act", bufs=3))
         psum = ctx.enter_context(tc.psum_pool(name="psum", bufs=1))
         ctx.enter_context(tc.manual_schedule())
 
         def is_model(n):
             return 0 <= n < MODELS
-
-        def matrices_of(step):
-            matrices = []
-            if is_model(step + 3):
-                matrices.append(2 * (step + 3))
-            if is_model(step + 1):
-                matrices.append(2 * (step + 1) + 1)
-            return matrices
 
         wraw = []
         wc = []
@@ -73,7 +63,6 @@ def tile_model_pa_kernel(tc, x, emb_W, emb_b, enc_W1, enc_b1, enc_W2, enc_b2, ou
         eb = const.tile([P, PACK], F32, name="eb")
         brows = const.tile([P, D], BF16, name="brows")
         b1T = const.tile([P, PACK, MODELS], F32, name="b1T")
-        b2T = const.tile([P, PACK, MODELS], BF16, name="b2T")
         b2bc = const.tile([P, MODELS, D], BF16, name="b2bc")
         warm = const.tile([P, 1], F32, name="warm")
         warm2 = const.tile([P, 1], F32, name="warm2")
@@ -94,39 +83,40 @@ def tile_model_pa_kernel(tc, x, emb_W, emb_b, enc_W1, enc_b1, enc_W2, enc_b2, ou
         x_v = x.rearrange("b c (l y) -> (b c) l y", l=2)
         nc.scalar.dma_start(out=eb_bf[:], in_=emb_b.rearrange("(p t) -> p t", t=PACK))
         nc.scalar.dma_start(out=brows[0:MODELS, :], in_=enc_b1)
-        nc.scalar.dma_start(out=brows[MODELS:2 * MODELS, :], in_=enc_b2)
         nc.sync.dma_start(out=embw[:], in_=emb_W)
         nc.sync.dma_start(out=x_sb[:, :, 0:FIRST_X_COLS], in_=x_v[:, :, 0:FIRST_X_COLS])
-        load_order = []
-        for step in range(FIRST_STEP, MODELS):
-            load_order.extend(matrices_of(step))
-        load_weights(load_order[0])
+        load_weights(0)
         nc.sync.dma_start(out=x_sb[:, :, FIRST_X_COLS:X_HALF], in_=x_v[:, :, FIRST_X_COLS:X_HALF])
-        for i in load_order[1:]:
+        for i in (2, 4, 1, 6):
             load_weights(i)
+        nc.sync.dma_start(
+            out=b2bc[:].rearrange("p n d -> p (n d)"),
+            in_=enc_b2.rearrange("n d -> (n d)").partition_broadcast(P),
+        )
+        for n in range(1, MODELS):
+            load_weights(2 * n + 1)
+            if is_model(n + 3):
+                load_weights(2 * (n + 3))
         nc.scalar.activation(out=warm2[:], in_=warm[:], func=GELU)
 
         wg = {}
         wgg = {}
 
-        def shares(i):
-            n = i // 2
-            if i % 2 == 0:
-                return (W1_SPLIT, D if n < GPSIMD_FROM else W1_SPLIT)
-            if n == 0 or n == MODELS - 1:
-                return (0, D)
-            return (D, D)
-
-        def w_regroup_scalar(i):
+        def w_tile(i):
             wg[i] = grp.tile([P, D, PACK], BF16, name="wg", tag="wg", align_bytes=64)
-            s_end = shares(i)[0]
-            if s_end > 0:
-                regroup(nc.scalar.copy, wg[i][:, 0:s_end, :], wraw[i][:, :, 0:s_end])
 
-        def w_regroup_vector(i):
-            s_end, v_end = shares(i)
-            if s_end < v_end:
-                regroup(nc.vector.tensor_copy, wg[i][:, s_end:v_end, :], wraw[i][:, :, s_end:v_end])
+        def w_regroup_scalar(i, c0, c1):
+            regroup(nc.scalar.copy, wg[i][:, c0:c1, :], wraw[i][:, :, c0:c1])
+
+        def gpsimd_copy(dst, i, c0, c1):
+            nc.gpsimd.tensor_scalar(
+                out=dst,
+                in0=wraw[i][:, :, c0:c1].rearrange("p t c -> p c t"),
+                scalar1=1.0,
+                scalar2=0.0,
+                op0=MULT,
+                op1=ADD,
+            )
 
         def quantise_cols(i, grouped, c0, width):
             nc.vector.quantize_mx(
@@ -136,26 +126,17 @@ def tile_model_pa_kernel(tc, x, emb_W, emb_b, enc_W1, enc_b1, enc_W2, enc_b2, ou
             )
 
         def w_quantise(i):
-            v_end = shares(i)[1]
-            quantise_cols(i, wg[i][:, 0:v_end, :], 0, v_end)
+            quantise_cols(i, wg[i][:], 0, D)
 
-        def w_regroup_gpsimd(i, first):
-            v_end = shares(i)[1]
-            wgg[i] = grp.tile([P, D - W1_SPLIT, PACK], BF16, name="wgg", tag="wgg", bufs=1, align_bytes=64)
-            if first:
-                nc.vector.memset(wgg[i][:, 0:HOLD_COLS, :], 0.0)
-            nc.gpsimd.tensor_scalar(
-                out=wgg[i][:],
-                in0=wraw[i][:, :, v_end:D].rearrange("p t c -> p c t"),
-                scalar1=1.0,
-                scalar2=0.0,
-                op0=MULT,
-                op1=ADD,
-            )
+        def w_quantise_scalar_half(i):
+            quantise_cols(i, wg[i][:, 0:HALF, :], 0, HALF)
+
+        def w_regroup_gpsimd(i):
+            wgg[i] = grp.tile([P, HALF, PACK], BF16, name="wgg", tag="wgg", bufs=1, align_bytes=64)
+            gpsimd_copy(wgg[i][:], i, HALF, D)
 
         def w_quantise_gpsimd(i):
-            v_end = shares(i)[1]
-            quantise_cols(i, wgg[i][:], v_end, D - v_end)
+            quantise_cols(i, wgg[i][:], HALF, HALF)
 
         def x_transpose(pair, bank, copy):
             x_ps = psum.tile([P, 4, P], BF16, name="x_ps", tag=bank)
@@ -178,14 +159,14 @@ def tile_model_pa_kernel(tc, x, emb_W, emb_b, enc_W1, enc_b1, enc_W2, enc_b2, ou
 
         def embed(n):
             for l in range(2):
-                e_ps[(n, l)] = psum.tile([P, PACK, P], F32, name="e_ps", tag="e%d" % l)
+                e_ps[(n, l)] = psum.tile([P, PACK, P], F32, name="e_ps", tag="%s%d" % ("eo"[n % 2], l))
                 for t in range(PACK):
                     nc.tensor.matmul(
                         e_ps[(n, l)][:, t, :], lhsT=embwp[:, t, :], rhs=xT[:, n, l, :], start=True, stop=True
                     )
 
         def e_out_of_psum(n):
-            ge[n] = act.tile([P, TOKENS, PACK], BF16, name="ge", tag="ge", align_bytes=64)
+            ge[n] = act.tile([P, TOKENS, PACK], BF16, name="ge", tag="ge", bufs=MODELS, align_bytes=64)
             for l in range(2):
                 nc.vector.tensor_tensor(
                     out=ge[n][:, l * P:(l + 1) * P, :],
@@ -240,9 +221,8 @@ def tile_model_pa_kernel(tc, x, emb_W, emb_b, enc_W1, enc_b1, enc_W2, enc_b2, ou
             )
 
         def layer2(n):
-            kind = "e" if (n >= LATE_OUTPUT_FROM and n % 2 == 1) else "o"
             for l in range(2):
-                o = psum.tile([P, D], F32, name="o_ps", tag="%s%d" % (kind, l))
+                o = psum.tile([P, D], F32, name="o_ps", tag="%s%d" % ("eo"[n % 2], l))
                 o_ps[(n, l)] = o
                 nc.tensor.matmul_mx(
                     out=o[:],
@@ -264,66 +244,79 @@ def tile_model_pa_kernel(tc, x, emb_W, emb_b, enc_W1, enc_b1, enc_W2, enc_b2, ou
             if not store_each_bank:
                 nc.sync.dma_start(out=dst, in_=o_sb[:])
 
-        def spread_b2(pair):
-            bb = psum.tile([P, 2, PACK, P], BF16, name="bb_ps", tag="o%d" % (pair % 2))
-            for nn in range(2):
-                for t in range(PACK):
-                    n = 2 * pair + nn
-                    nc.tensor.transpose(bb[:, nn, t, :], b2T[:, t, n:n + 1].to_broadcast([P, P]), ident[:])
-            nc.scalar.copy(
-                out=b2bc[:, 2 * pair:2 * pair + 2, :].rearrange("p n d -> p (n d)"),
-                in_=bb[:].rearrange("p n t c -> p (n t c)"),
-            )
-
         nc.vector.tensor_copy(out=embwp[:], in_=embw[:].rearrange("p (m t) -> p t m", t=PACK))
         nc.vector.tensor_copy(out=eb[:], in_=eb_bf[:])
-        x_transpose(0, "e0", nc.vector.tensor_copy)
-        bt_ps = psum.tile([P, PACK, P], BF16, name="bt_ps", tag="a3")
+        x_transpose(0, "a0", nc.vector.tensor_copy)
+        embed(0)
+        embed(1)
+        e_out_of_psum(0)
+        for i in (0, 2, 4, 1, 6):
+            w_tile(i)
+        w_regroup_scalar(0, 0, HALF)
+        x_transpose(1, "a1", nc.scalar.copy)
+        x_transpose(2, "a2", nc.scalar.copy)
+        x_transpose(3, "a3", nc.scalar.copy)
+        w_regroup_scalar(2, 0, HALF)
+        w_regroup_scalar(4, 0, HALF)
+        w_regroup_scalar(1, 0, HALF)
+        for i in (0, 2, 4, 1, 6):
+            gpsimd_copy(wg[i][:, HALF:D, :], i, HALF, D)
+        bt_ps = psum.tile([P, PACK, P], BF16, name="bt_ps", tag="a0")
         for t in range(PACK):
             nc.tensor.transpose(bt_ps[:, t, :], brows[:, t * P:(t + 1) * P], ident[:])
         nc.vector.tensor_copy(out=b1T[:], in_=bt_ps[:, :, 0:MODELS])
-        nc.vector.tensor_copy(out=b2T[:], in_=bt_ps[:, :, MODELS:2 * MODELS])
-        embed(0)
-        w_regroup_scalar(0)
-        x_transpose(1, "a0", nc.scalar.copy)
-        x_transpose(2, "a1", nc.scalar.copy)
-        x_transpose(3, "a2", nc.scalar.copy)
+        for n in range(1, E_FIRST):
+            embed(n + 1)
+            e_out_of_psum(n)
+        w_quantise(0)
+        e_quantise(0)
+        layer1(0)
+        w_quantise(2)
+        e_quantise(1)
+        layer1(1)
+        gelu(0)
+        w_regroup_scalar(6, 0, HALF)
+        for n in range(E_FIRST, MODELS):
+            if is_model(n + 1):
+                embed(n + 1)
+            e_out_of_psum(n)
+        w_quantise(4)
 
-        for step in range(FIRST_STEP, MODELS):
-            matrices = matrices_of(step)
+        for step in range(MODELS):
             if is_model(step + 1):
                 gelu(step + 1)
                 if step + 1 >= SCALAR_REGROUPS_G_FROM:
                     g_regroup(step + 1, nc.scalar.copy)
-            for i in matrices:
-                if i > 0:
-                    w_regroup_scalar(i)
-            if step in (-2, -1):
-                spread_b2(2 * (step + 2))
-                spread_b2(2 * (step + 2) + 1)
+                i = 2 * (step + 1) + 1
+                w_tile(i)
+                w_regroup_scalar(i, 0, HALF if step + 1 >= MODELS - 2 else D)
+            if is_model(step + 4):
+                i = 2 * (step + 4)
+                w_tile(i)
+                w_regroup_scalar(i, 0, HALF)
             if is_model(step + 2):
                 e_quantise(step + 2)
                 layer1(step + 2)
-            for i in matrices:
-                w_regroup_vector(i)
-            if is_model(step):
-                if step < SCALAR_REGROUPS_G_FROM:
-                    g_regroup(step, nc.vector.tensor_copy)
+            if step < SCALAR_REGROUPS_G_FROM:
+                g_regroup(step, nc.vector.tensor_copy)
+            if step >= MODELS - 2:
+                w_quantise_scalar_half(2 * step + 1)
+            else:
                 w_quantise(2 * step + 1)
-                g_quantise(step)
-                layer2(step)
-            if is_model(step + 3):
+            g_quantise(step)
+            layer2(step)
+            if step + 3 < GPSIMD_EARLY:
                 w_quantise(2 * (step + 3))
-                if step + 3 >= GPSIMD_FROM:
-                    w_quantise_gpsimd(2 * (step + 3))
-            ahead = step + GPSIMD_LEAD
-            if is_model(ahead) and ahead >= GPSIMD_FROM:
-                w_regroup_gpsimd(2 * ahead, ahead == GPSIMD_FROM)
-            if is_model(step + 3):
-                e_out_of_psum(step + 3)
+            elif is_model(step + 3):
+                w_quantise_scalar_half(2 * (step + 3))
+                w_quantise_gpsimd(2 * (step + 3))
+            elif step + 1 in (MODELS - 2, MODELS - 1):
+                w_quantise_gpsimd(2 * (step + 1) + 1)
             if is_model(step + 4):
-                embed(step + 4)
-            if is_model(step) and step < LATE_OUTPUT_FROM:
+                w_regroup_gpsimd(2 * (step + 4))
+            elif step + 2 in (MODELS - 2, MODELS - 1):
+                w_regroup_gpsimd(2 * (step + 2) + 1)
+            if step < LATE_OUTPUT_FROM:
                 output(step, False)
             if step > LATE_OUTPUT_FROM:
                 output(step - 1, False)

@@ -22,8 +22,8 @@ FLOPS = 2 * 2048 * 128 * 512 + 2 * 2 * 2048 * 512 * 512
 HALF = D // 2
 GPSIMD_EARLY = 4
 LATE_OUTPUT_FROM = MODELS - 2
-SCALAR_REGROUPS_G_FROM = MODELS - 2
-E_FIRST = 4
+VECTOR_W1 = (5,)
+B2_AFTER = 2
 X_HALF = 1024
 FIRST_X_COLS = 2 * P
 
@@ -41,7 +41,7 @@ def tile_model_pa_kernel(tc, x, emb_W, emb_b, enc_W1, enc_b1, enc_W2, enc_b2, ou
         const = ctx.enter_context(tc.tile_pool(name="const", bufs=1))
         wraw_pool = ctx.enter_context(tc.tile_pool(name="wraw", bufs=1))
         wq_pool = ctx.enter_context(tc.tile_pool(name="wq", bufs=1))
-        grp = ctx.enter_context(tc.tile_pool(name="grp", bufs=5))
+        grp = ctx.enter_context(tc.tile_pool(name="grp", bufs=8))
         act = ctx.enter_context(tc.tile_pool(name="act", bufs=3))
         psum = ctx.enter_context(tc.psum_pool(name="psum", bufs=1))
         ctx.enter_context(tc.manual_schedule())
@@ -85,16 +85,16 @@ def tile_model_pa_kernel(tc, x, emb_W, emb_b, enc_W1, enc_b1, enc_W2, enc_b2, ou
         nc.scalar.dma_start(out=brows[0:MODELS, :], in_=enc_b1)
         nc.sync.dma_start(out=embw[:], in_=emb_W)
         nc.sync.dma_start(out=x_sb[:, :, 0:FIRST_X_COLS], in_=x_v[:, :, 0:FIRST_X_COLS])
-        load_weights(0)
         nc.sync.dma_start(out=x_sb[:, :, FIRST_X_COLS:X_HALF], in_=x_v[:, :, FIRST_X_COLS:X_HALF])
-        for i in (2, 4, 1, 6):
+        for i in (0, 2, 4, 1, 6):
             load_weights(i)
-        nc.sync.dma_start(
-            out=b2bc[:].rearrange("p n d -> p (n d)"),
-            in_=enc_b2.rearrange("n d -> (n d)").partition_broadcast(P),
-        )
         for n in range(1, MODELS):
             load_weights(2 * n + 1)
+            if n == B2_AFTER:
+                nc.sync.dma_start(
+                    out=b2bc[:].rearrange("p n d -> p (n d)"),
+                    in_=enc_b2.rearrange("n d -> (n d)").partition_broadcast(P),
+                )
             if is_model(n + 3):
                 load_weights(2 * (n + 3))
         nc.scalar.activation(out=warm2[:], in_=warm[:], func=GELU)
@@ -107,6 +107,20 @@ def tile_model_pa_kernel(tc, x, emb_W, emb_b, enc_W1, enc_b1, enc_W2, enc_b2, ou
 
         def w_regroup_scalar(i, c0, c1):
             regroup(nc.scalar.copy, wg[i][:, c0:c1, :], wraw[i][:, :, c0:c1])
+
+        def w_regroup_tensor(i, bank):
+            w_ps = psum.tile([P, HALF, PACK], BF16, name="w_ps", tag=bank)
+            for c0 in range(0, HALF, P):
+                nc.tensor.matmul(
+                    w_ps[:, c0:c0 + P, :].rearrange("p c t -> p (c t)"),
+                    lhsT=ident[:],
+                    rhs=wraw[i][:, :, c0:c0 + P].rearrange("p t c -> p c t"),
+                    start=True,
+                    stop=True,
+                )
+            nc.scalar.copy(
+                out=wg[i][:, 0:HALF, :].rearrange("p c t -> p (c t)"), in_=w_ps[:].rearrange("p c t -> p (c t)")
+            )
 
         def gpsimd_copy(dst, i, c0, c1):
             nc.gpsimd.tensor_scalar(
@@ -244,67 +258,64 @@ def tile_model_pa_kernel(tc, x, emb_W, emb_b, enc_W1, enc_b1, enc_W2, enc_b2, ou
             if not store_each_bank:
                 nc.sync.dma_start(out=dst, in_=o_sb[:])
 
+        for i in (0, 2, 4, 1, 6):
+            w_tile(i)
         nc.vector.tensor_copy(out=embwp[:], in_=embw[:].rearrange("p (m t) -> p t m", t=PACK))
         nc.vector.tensor_copy(out=eb[:], in_=eb_bf[:])
         x_transpose(0, "a0", nc.vector.tensor_copy)
         embed(0)
+        x_transpose(1, "a2", nc.scalar.copy)
+        x_transpose(2, "a3", nc.scalar.copy)
+        x_transpose(3, "a0", nc.scalar.copy)
         embed(1)
-        e_out_of_psum(0)
-        for i in (0, 2, 4, 1, 6):
-            w_tile(i)
-        w_regroup_scalar(0, 0, HALF)
-        x_transpose(1, "a1", nc.scalar.copy)
-        x_transpose(2, "a2", nc.scalar.copy)
-        x_transpose(3, "a3", nc.scalar.copy)
-        w_regroup_scalar(2, 0, HALF)
-        w_regroup_scalar(4, 0, HALF)
-        w_regroup_scalar(1, 0, HALF)
         for i in (0, 2, 4, 1, 6):
             gpsimd_copy(wg[i][:, HALF:D, :], i, HALF, D)
+        early = ((0, "a1"), (2, "a2"), (4, "a3"), (1, "a1"))
+        for n in range(MODELS):
+            e_out_of_psum(n)
+            if n < len(early):
+                w_regroup_tensor(*early[n])
+            if is_model(n + 2):
+                embed(n + 2)
         bt_ps = psum.tile([P, PACK, P], BF16, name="bt_ps", tag="a0")
         for t in range(PACK):
             nc.tensor.transpose(bt_ps[:, t, :], brows[:, t * P:(t + 1) * P], ident[:])
         nc.vector.tensor_copy(out=b1T[:], in_=bt_ps[:, :, 0:MODELS])
-        for n in range(1, E_FIRST):
-            embed(n + 1)
-            e_out_of_psum(n)
-        w_quantise(0)
-        e_quantise(0)
-        layer1(0)
-        w_quantise(2)
-        e_quantise(1)
-        layer1(1)
-        gelu(0)
-        w_regroup_scalar(6, 0, HALF)
-        for n in range(E_FIRST, MODELS):
-            if is_model(n + 1):
-                embed(n + 1)
-            e_out_of_psum(n)
+        for n in range(2):
+            w_quantise(2 * n)
+            e_quantise(n)
+            layer1(n)
         w_quantise(4)
+        w_regroup_scalar(6, 0, HALF)
+        w_tile(3)
+        w_regroup_scalar(3, 0, D)
+        gelu(0)
 
         for step in range(MODELS):
             if is_model(step + 1):
                 gelu(step + 1)
-                if step + 1 >= SCALAR_REGROUPS_G_FROM:
-                    g_regroup(step + 1, nc.scalar.copy)
-                i = 2 * (step + 1) + 1
-                w_tile(i)
-                w_regroup_scalar(i, 0, HALF if step + 1 >= MODELS - 2 else D)
             if is_model(step + 4):
                 i = 2 * (step + 4)
                 w_tile(i)
-                w_regroup_scalar(i, 0, HALF)
+                if step + 4 not in VECTOR_W1:
+                    w_regroup_scalar(i, 0, HALF)
+            if is_model(step + 2):
+                i = 2 * (step + 2) + 1
+                w_tile(i)
+                w_regroup_scalar(i, 0, HALF if step + 2 >= MODELS - 2 else D)
             if is_model(step + 2):
                 e_quantise(step + 2)
                 layer1(step + 2)
-            if step < SCALAR_REGROUPS_G_FROM:
-                g_regroup(step, nc.vector.tensor_copy)
+            g_regroup(step, nc.vector.tensor_copy)
             if step >= MODELS - 2:
                 w_quantise_scalar_half(2 * step + 1)
             else:
                 w_quantise(2 * step + 1)
             g_quantise(step)
             layer2(step)
+            if step + 4 in VECTOR_W1:
+                i = 2 * (step + 4)
+                regroup(nc.vector.tensor_copy, wg[i][:, 0:HALF, :], wraw[i][:, :, 0:HALF])
             if step + 3 < GPSIMD_EARLY:
                 w_quantise(2 * (step + 3))
             elif is_model(step + 3):

@@ -108,20 +108,6 @@ def tile_model_pa_kernel(tc, x, emb_W, emb_b, enc_W1, enc_b1, enc_W2, enc_b2, ou
         def w_regroup_scalar(i, c0, c1):
             regroup(nc.scalar.copy, wg[i][:, c0:c1, :], wraw[i][:, :, c0:c1])
 
-        def w_regroup_tensor(i, bank):
-            w_ps = psum.tile([P, HALF, PACK], BF16, name="w_ps", tag=bank)
-            for c0 in range(0, HALF, P):
-                nc.tensor.matmul(
-                    w_ps[:, c0:c0 + P, :].rearrange("p c t -> p (c t)"),
-                    lhsT=ident[:],
-                    rhs=wraw[i][:, :, c0:c0 + P].rearrange("p t c -> p c t"),
-                    start=True,
-                    stop=True,
-                )
-            nc.scalar.copy(
-                out=wg[i][:, 0:HALF, :].rearrange("p c t -> p (c t)"), in_=w_ps[:].rearrange("p c t -> p (c t)")
-            )
-
         def gpsimd_copy(dst, i, c0, c1):
             nc.gpsimd.tensor_scalar(
                 out=dst,
@@ -269,12 +255,10 @@ def tile_model_pa_kernel(tc, x, emb_W, emb_b, enc_W1, enc_b1, enc_W2, enc_b2, ou
         x_transpose(3, "a0", nc.scalar.copy)
         embed(1)
         for i in (0, 2, 4, 1, 6):
+            w_regroup_scalar(i, 0, HALF)
             gpsimd_copy(wg[i][:, HALF:D, :], i, HALF, D)
-        early = ((0, "a1"), (2, "a2"), (4, "a3"), (1, "a1"))
         for n in range(MODELS):
             e_out_of_psum(n)
-            if n < len(early):
-                w_regroup_tensor(*early[n])
             if is_model(n + 2):
                 embed(n + 2)
         bt_ps = psum.tile([P, PACK, P], BF16, name="bt_ps", tag="a0")
@@ -286,7 +270,6 @@ def tile_model_pa_kernel(tc, x, emb_W, emb_b, enc_W1, enc_b1, enc_W2, enc_b2, ou
             e_quantise(n)
             layer1(n)
         w_quantise(4)
-        w_regroup_scalar(6, 0, HALF)
         w_tile(3)
         w_regroup_scalar(3, 0, D)
         gelu(0)

@@ -22,6 +22,7 @@ FLOPS = 2 * 2048 * 128 * 512 + 2 * 2 * 2048 * 512 * 512
 HALF = D // 2
 GPSIMD_EARLY = 4
 LATE_OUTPUT_FROM = MODELS - 2
+SCALAR_REGROUPS_G_FROM = MODELS - 1
 VECTOR_W1 = (5,)
 B2_AFTER = 2
 X_HALF = 1024
@@ -138,13 +139,13 @@ def tile_model_pa_kernel(tc, x, emb_W, emb_b, enc_W1, enc_b1, enc_W2, enc_b2, ou
         def w_quantise_gpsimd(i):
             quantise_cols(i, wgg[i][:], HALF, HALF)
 
-        def x_transpose(pair, bank, copy):
-            x_ps = psum.tile([P, 4, P], BF16, name="x_ps", tag=bank)
-            for nn in range(2):
+        def x_transpose(n0, count, bank, copy):
+            x_ps = psum.tile([P, 2 * count, P], BF16, name="x_ps", tag=bank)
+            for nn in range(count):
                 for l in range(2):
-                    c0 = (2 * pair + nn) * P
+                    c0 = (n0 + nn) * P
                     nc.tensor.transpose(x_ps[:, 2 * nn + l, :], x_sb[:, l, c0:c0 + P], ident[:])
-            copy(out=xT[:, 2 * pair:2 * pair + 2, :, :].rearrange("p n l c -> p (n l) c"), in_=x_ps[:])
+            copy(out=xT[:, n0:n0 + count, :, :].rearrange("p n l c -> p (n l) c"), in_=x_ps[:])
 
         e_ps = {}
         ge = {}
@@ -234,33 +235,41 @@ def tile_model_pa_kernel(tc, x, emb_W, emb_b, enc_W1, enc_b1, enc_W2, enc_b2, ou
                     stop=True,
                 )
 
-        def output(n, store_each_bank):
+        def output(n, store_each_piece):
             o_sb = act.tile([P, 2, D], F32, name="o_sb", tag="o_sb")
             dst = out[n].rearrange("b c l d -> (b c) l d")
             for l in range(2):
-                nc.vector.tensor_tensor(out=o_sb[:, l, :], in0=o_ps[(n, l)][:], in1=b2bc[:, n, :], op=ADD)
-                if store_each_bank:
-                    nc.sync.dma_start(out=dst[:, l, :], in_=o_sb[:, l, :])
-            if not store_each_bank:
+                width = HALF if (store_each_piece and l == 1) else D
+                for d0 in range(0, D, width):
+                    cols = slice(d0, d0 + width)
+                    nc.vector.tensor_tensor(
+                        out=o_sb[:, l, cols], in0=o_ps[(n, l)][:, cols], in1=b2bc[:, n, cols], op=ADD
+                    )
+                    if store_each_piece:
+                        nc.sync.dma_start(out=dst[:, l, cols], in_=o_sb[:, l, cols])
+            if not store_each_piece:
                 nc.sync.dma_start(out=dst, in_=o_sb[:])
 
         for i in (0, 2, 4, 1, 6):
             w_tile(i)
         nc.vector.tensor_copy(out=embwp[:], in_=embw[:].rearrange("p (m t) -> p t m", t=PACK))
         nc.vector.tensor_copy(out=eb[:], in_=eb_bf[:])
-        x_transpose(0, "a0", nc.vector.tensor_copy)
+        x_transpose(0, 1, "a0", nc.vector.tensor_copy)
+        x_transpose(1, 1, "a1", nc.scalar.copy)
         embed(0)
-        x_transpose(1, "a2", nc.scalar.copy)
-        x_transpose(2, "a3", nc.scalar.copy)
-        x_transpose(3, "a0", nc.scalar.copy)
         embed(1)
+        x_transpose(2, 2, "a2", nc.scalar.copy)
         for i in (0, 2, 4, 1, 6):
-            w_regroup_scalar(i, 0, HALF)
             gpsimd_copy(wg[i][:, HALF:D, :], i, HALF, D)
+        early = (0, 2, 4, 1, 6)
         for n in range(MODELS):
             e_out_of_psum(n)
             if is_model(n + 2):
                 embed(n + 2)
+            if n < 2:
+                x_transpose(4 + 2 * n, 2, "a%d" % (3 * (1 - n)), nc.scalar.copy)
+            if n < len(early):
+                w_regroup_scalar(early[n], 0, HALF)
         bt_ps = psum.tile([P, PACK, P], BF16, name="bt_ps", tag="a0")
         for t in range(PACK):
             nc.tensor.transpose(bt_ps[:, t, :], brows[:, t * P:(t + 1) * P], ident[:])
@@ -271,12 +280,15 @@ def tile_model_pa_kernel(tc, x, emb_W, emb_b, enc_W1, enc_b1, enc_W2, enc_b2, ou
             layer1(n)
         w_quantise(4)
         w_tile(3)
-        w_regroup_scalar(3, 0, D)
+        w_regroup_scalar(3, 0, HALF)
         gelu(0)
+        w_regroup_scalar(3, HALF, D)
 
         for step in range(MODELS):
             if is_model(step + 1):
                 gelu(step + 1)
+                if step + 1 >= SCALAR_REGROUPS_G_FROM:
+                    g_regroup(step + 1, nc.scalar.copy)
             if is_model(step + 4):
                 i = 2 * (step + 4)
                 w_tile(i)
@@ -289,7 +301,8 @@ def tile_model_pa_kernel(tc, x, emb_W, emb_b, enc_W1, enc_b1, enc_W2, enc_b2, ou
             if is_model(step + 2):
                 e_quantise(step + 2)
                 layer1(step + 2)
-            g_regroup(step, nc.vector.tensor_copy)
+            if step < SCALAR_REGROUPS_G_FROM:
+                g_regroup(step, nc.vector.tensor_copy)
             if step >= MODELS - 2:
                 w_quantise_scalar_half(2 * step + 1)
             else:

@@ -23,8 +23,8 @@ HALF = D // 2
 GPSIMD_EARLY = 4
 LATE_OUTPUT_FROM = MODELS - 2
 SCALAR_REGROUPS_G_FROM = MODELS - 1
-VECTOR_W1 = (5,)
 B2_AFTER = 2
+HOLD_COLS = 8
 X_HALF = 1024
 FIRST_X_COLS = 2 * P
 
@@ -86,8 +86,10 @@ def tile_model_pa_kernel(tc, x, emb_W, emb_b, enc_W1, enc_b1, enc_W2, enc_b2, ou
         nc.scalar.dma_start(out=brows[0:MODELS, :], in_=enc_b1)
         nc.sync.dma_start(out=embw[:], in_=emb_W)
         nc.sync.dma_start(out=x_sb[:, :, 0:FIRST_X_COLS], in_=x_v[:, :, 0:FIRST_X_COLS])
-        nc.sync.dma_start(out=x_sb[:, :, FIRST_X_COLS:X_HALF], in_=x_v[:, :, FIRST_X_COLS:X_HALF])
-        for i in (0, 2, 4, 1, 6):
+        nc.sync.dma_start(out=x_sb[:, :, FIRST_X_COLS:X_HALF // 2], in_=x_v[:, :, FIRST_X_COLS:X_HALF // 2])
+        load_weights(0)
+        nc.sync.dma_start(out=x_sb[:, :, X_HALF // 2:X_HALF], in_=x_v[:, :, X_HALF // 2:X_HALF])
+        for i in (2, 4, 1, 6):
             load_weights(i)
         for n in range(1, MODELS):
             load_weights(2 * n + 1)
@@ -108,6 +110,24 @@ def tile_model_pa_kernel(tc, x, emb_W, emb_b, enc_W1, enc_b1, enc_W2, enc_b2, ou
 
         def w_regroup_scalar(i, c0, c1):
             regroup(nc.scalar.copy, wg[i][:, c0:c1, :], wraw[i][:, :, c0:c1])
+
+        w_ps = {}
+
+        def w_regroup_tensor(i):
+            w_ps[i] = psum.tile([P, HALF, PACK], BF16, name="w_ps", tag="e%d" % (i // 2 % 2))
+            for c0 in range(0, HALF, P):
+                nc.tensor.matmul(
+                    w_ps[i][:, c0:c0 + P, :].rearrange("p c t -> p (c t)"),
+                    lhsT=ident[:],
+                    rhs=wraw[i][:, :, c0:c0 + P].rearrange("p t c -> p c t"),
+                    start=True,
+                    stop=True,
+                )
+
+        def w_out_of_psum(i):
+            nc.scalar.copy(
+                out=wg[i][:, 0:HALF, :].rearrange("p c t -> p (c t)"), in_=w_ps[i][:].rearrange("p c t -> p (c t)")
+            )
 
         def gpsimd_copy(dst, i, c0, c1):
             nc.gpsimd.tensor_scalar(
@@ -132,8 +152,13 @@ def tile_model_pa_kernel(tc, x, emb_W, emb_b, enc_W1, enc_b1, enc_W2, enc_b2, ou
         def w_quantise_scalar_half(i):
             quantise_cols(i, wg[i][:, 0:HALF, :], 0, HALF)
 
-        def w_regroup_gpsimd(i):
+        def w_hold_gpsimd(i):
             wgg[i] = grp.tile([P, HALF, PACK], BF16, name="wgg", tag="wgg", bufs=1, align_bytes=64)
+            nc.vector.memset(wgg[i][:, 0:HOLD_COLS, :], 0.0)
+
+        def w_regroup_gpsimd(i):
+            if i not in wgg:
+                wgg[i] = grp.tile([P, HALF, PACK], BF16, name="wgg", tag="wgg", bufs=1, align_bytes=64)
             gpsimd_copy(wgg[i][:], i, HALF, D)
 
         def w_quantise_gpsimd(i):
@@ -223,7 +248,7 @@ def tile_model_pa_kernel(tc, x, emb_W, emb_b, enc_W1, enc_b1, enc_W2, enc_b2, ou
 
         def layer2(n):
             for l in range(2):
-                o = psum.tile([P, D], F32, name="o_ps", tag="%s%d" % ("eo"[n % 2], l))
+                o = psum.tile([P, D], F32, name="o_ps", tag="%s%d" % ("e" if n == MODELS - 1 else "o", l))
                 o_ps[(n, l)] = o
                 nc.tensor.matmul_mx(
                     out=o[:],
@@ -266,10 +291,10 @@ def tile_model_pa_kernel(tc, x, emb_W, emb_b, enc_W1, enc_b1, enc_W2, enc_b2, ou
             e_out_of_psum(n)
             if is_model(n + 2):
                 embed(n + 2)
-            if n < 2:
-                x_transpose(4 + 2 * n, 2, "a%d" % (3 * (1 - n)), nc.scalar.copy)
             if n < len(early):
                 w_regroup_scalar(early[n], 0, HALF)
+            if n < 2:
+                x_transpose(4 + 2 * n, 2, "a%d" % (3 * (1 - n)), nc.scalar.copy)
         bt_ps = psum.tile([P, PACK, P], BF16, name="bt_ps", tag="a0")
         for t in range(PACK):
             nc.tensor.transpose(bt_ps[:, t, :], brows[:, t * P:(t + 1) * P], ident[:])
@@ -279,6 +304,7 @@ def tile_model_pa_kernel(tc, x, emb_W, emb_b, enc_W1, enc_b1, enc_W2, enc_b2, ou
             e_quantise(n)
             layer1(n)
         w_quantise(4)
+        w_regroup_tensor(2 * GPSIMD_EARLY)
         w_tile(3)
         w_regroup_scalar(3, 0, HALF)
         gelu(0)
@@ -290,10 +316,8 @@ def tile_model_pa_kernel(tc, x, emb_W, emb_b, enc_W1, enc_b1, enc_W2, enc_b2, ou
                 if step + 1 >= SCALAR_REGROUPS_G_FROM:
                     g_regroup(step + 1, nc.scalar.copy)
             if is_model(step + 4):
-                i = 2 * (step + 4)
-                w_tile(i)
-                if step + 4 not in VECTOR_W1:
-                    w_regroup_scalar(i, 0, HALF)
+                w_tile(2 * (step + 4))
+                w_out_of_psum(2 * (step + 4))
             if is_model(step + 2):
                 i = 2 * (step + 2) + 1
                 w_tile(i)
@@ -307,18 +331,18 @@ def tile_model_pa_kernel(tc, x, emb_W, emb_b, enc_W1, enc_b1, enc_W2, enc_b2, ou
                 w_quantise_scalar_half(2 * step + 1)
             else:
                 w_quantise(2 * step + 1)
+            if step + 1 in (MODELS - 2, MODELS - 1):
+                w_quantise_gpsimd(2 * (step + 1) + 1)
             g_quantise(step)
             layer2(step)
-            if step + 4 in VECTOR_W1:
-                i = 2 * (step + 4)
-                regroup(nc.vector.tensor_copy, wg[i][:, 0:HALF, :], wraw[i][:, :, 0:HALF])
+            if is_model(step + 5):
+                w_regroup_tensor(2 * (step + 5))
             if step + 3 < GPSIMD_EARLY:
+                w_hold_gpsimd(2 * (step + 4))
                 w_quantise(2 * (step + 3))
             elif is_model(step + 3):
-                w_quantise_scalar_half(2 * (step + 3))
                 w_quantise_gpsimd(2 * (step + 3))
-            elif step + 1 in (MODELS - 2, MODELS - 1):
-                w_quantise_gpsimd(2 * (step + 1) + 1)
+                w_quantise_scalar_half(2 * (step + 3))
             if is_model(step + 4):
                 w_regroup_gpsimd(2 * (step + 4))
             elif step + 2 in (MODELS - 2, MODELS - 1):

@@ -23,7 +23,7 @@ HALF = D // 2
 GPSIMD_EARLY = 4
 LATE_OUTPUT_FROM = MODELS - 2
 SCALAR_REGROUPS_G_FROM = MODELS - 1
-B2_AFTER = 2
+E_EARLY = 2 * MODELS - 3
 HOLD_COLS = 8
 X_HALF = 1024
 FIRST_X_COLS = 2 * P
@@ -93,13 +93,13 @@ def tile_model_pa_kernel(tc, x, emb_W, emb_b, enc_W1, enc_b1, enc_W2, enc_b2, ou
             load_weights(i)
         for n in range(1, MODELS):
             load_weights(2 * n + 1)
-            if n == B2_AFTER:
-                nc.sync.dma_start(
-                    out=b2bc[:].rearrange("p n d -> p (n d)"),
-                    in_=enc_b2.rearrange("n d -> (n d)").partition_broadcast(P),
-                )
             if is_model(n + 3):
                 load_weights(2 * (n + 3))
+            if n % 2 == 1:
+                nc.sync.dma_start(
+                    out=b2bc[:, n - 1:n + 1, :].rearrange("p n d -> p (n d)"),
+                    in_=enc_b2[n - 1:n + 1, :].rearrange("n d -> (n d)").partition_broadcast(P),
+                )
         nc.scalar.activation(out=warm2[:], in_=warm[:], func=GELU)
 
         wg = {}
@@ -114,7 +114,7 @@ def tile_model_pa_kernel(tc, x, emb_W, emb_b, enc_W1, enc_b1, enc_W2, enc_b2, ou
         w_ps = {}
 
         def w_regroup_tensor(i):
-            w_ps[i] = psum.tile([P, HALF, PACK], BF16, name="w_ps", tag="e%d" % (i // 2 % 2))
+            w_ps[i] = psum.tile([P, HALF, PACK], BF16, name="w_ps", tag="e1")
             for c0 in range(0, HALF, P):
                 nc.tensor.matmul(
                     w_ps[i][:, c0:c0 + P, :].rearrange("p c t -> p (c t)"),
@@ -183,23 +183,23 @@ def tile_model_pa_kernel(tc, x, emb_W, emb_b, enc_W1, enc_b1, enc_W2, enc_b2, ou
         gs = {}
         o_ps = {}
 
-        def embed(n):
-            for l in range(2):
-                e_ps[(n, l)] = psum.tile([P, PACK, P], F32, name="e_ps", tag="%s%d" % ("eo"[n % 2], l))
-                for t in range(PACK):
-                    nc.tensor.matmul(
-                        e_ps[(n, l)][:, t, :], lhsT=embwp[:, t, :], rhs=xT[:, n, l, :], start=True, stop=True
-                    )
-
-        def e_out_of_psum(n):
-            ge[n] = act.tile([P, TOKENS, PACK], BF16, name="ge", tag="ge", bufs=MODELS, align_bytes=64)
-            for l in range(2):
-                nc.vector.tensor_tensor(
-                    out=ge[n][:, l * P:(l + 1) * P, :],
-                    in0=e_ps[(n, l)][:].rearrange("p t c -> p c t"),
-                    in1=eb[:].unsqueeze(1).to_broadcast([P, P, PACK]),
-                    op=ADD,
+        def embed(half, bank):
+            e_ps[half] = psum.tile([P, PACK, P], F32, name="e_ps", tag=bank)
+            for t in range(PACK):
+                nc.tensor.matmul(
+                    e_ps[half][:, t, :], lhsT=embwp[:, t, :], rhs=xT[:, half // 2, half % 2, :], start=True, stop=True
                 )
+
+        def e_out_of_psum(half):
+            n, l = divmod(half, 2)
+            if l == 0:
+                ge[n] = act.tile([P, TOKENS, PACK], BF16, name="ge", tag="ge", bufs=MODELS, align_bytes=64)
+            nc.vector.tensor_tensor(
+                out=ge[n][:, l * P:(l + 1) * P, :],
+                in0=e_ps[half][:].rearrange("p t c -> p c t"),
+                in1=eb[:].unsqueeze(1).to_broadcast([P, P, PACK]),
+                op=ADD,
+            )
 
         def e_quantise(n):
             ec[n] = act.tile([P, TOKENS], U32, name="ec", tag="ec", align_bytes=64)
@@ -209,6 +209,9 @@ def tile_model_pa_kernel(tc, x, emb_W, emb_b, enc_W1, enc_b1, enc_W2, enc_b2, ou
                 scales=es[n][:],
                 in_=ge[n][:].rearrange("p c t -> p (c t)"),
             )
+
+        def e_bank(half):
+            return ("e0", "e1", "o0", "o1")[half % 4]
 
         def layer1(n):
             for t_hi in range(2):
@@ -261,7 +264,7 @@ def tile_model_pa_kernel(tc, x, emb_W, emb_b, enc_W1, enc_b1, enc_W2, enc_b2, ou
                 )
 
         def output(n, store_each_piece):
-            o_sb = act.tile([P, 2, D], F32, name="o_sb", tag="o_sb")
+            o_sb = act.tile([P, 2, D], F32, name="o_sb", tag="o_sb", bufs=8)
             dst = out[n].rearrange("b c l d -> (b c) l d")
             for l in range(2):
                 width = HALF if (store_each_piece and l == 1) else D
@@ -281,16 +284,19 @@ def tile_model_pa_kernel(tc, x, emb_W, emb_b, enc_W1, enc_b1, enc_W2, enc_b2, ou
         nc.vector.tensor_copy(out=eb[:], in_=eb_bf[:])
         x_transpose(0, 1, "a0", nc.vector.tensor_copy)
         x_transpose(1, 1, "a1", nc.scalar.copy)
-        embed(0)
-        embed(1)
+        for half in range(4):
+            embed(half, e_bank(half))
         x_transpose(2, 2, "a2", nc.scalar.copy)
         for i in (0, 2, 4, 1, 6):
             gpsimd_copy(wg[i][:, HALF:D, :], i, HALF, D)
         early = (0, 2, 4, 1, 6)
         for n in range(MODELS):
-            e_out_of_psum(n)
-            if is_model(n + 2):
-                embed(n + 2)
+            for half in (2 * n, 2 * n + 1):
+                if half < E_EARLY:
+                    e_out_of_psum(half)
+            for half in (2 * n + 4, 2 * n + 5):
+                if half < E_EARLY:
+                    embed(half, e_bank(half))
             if n < len(early):
                 w_regroup_scalar(early[n], 0, HALF)
             if n < 2:
@@ -322,6 +328,9 @@ def tile_model_pa_kernel(tc, x, emb_W, emb_b, enc_W1, enc_b1, enc_W2, enc_b2, ou
                 i = 2 * (step + 2) + 1
                 w_tile(i)
                 w_regroup_scalar(i, 0, HALF if step + 2 >= MODELS - 2 else D)
+            late_half = E_EARLY + step - 1
+            if E_EARLY <= late_half < 2 * MODELS:
+                embed(late_half, "e0")
             if is_model(step + 2):
                 e_quantise(step + 2)
                 layer1(step + 2)
@@ -347,6 +356,8 @@ def tile_model_pa_kernel(tc, x, emb_W, emb_b, enc_W1, enc_b1, enc_W2, enc_b2, ou
                 w_regroup_gpsimd(2 * (step + 4))
             elif step + 2 in (MODELS - 2, MODELS - 1):
                 w_regroup_gpsimd(2 * (step + 2) + 1)
+            if E_EARLY <= late_half < 2 * MODELS:
+                e_out_of_psum(late_half)
             if step < LATE_OUTPUT_FROM:
                 output(step, False)
             if step > LATE_OUTPUT_FROM:

@@ -24,6 +24,7 @@ GPSIMD_EARLY = 4
 LATE_OUTPUT_FROM = MODELS - 2
 SCALAR_REGROUPS_G_FROM = MODELS - 1
 E_EARLY = 2 * MODELS - 3
+RUN = 8
 HOLD_COLS = 8
 X_HALF = 1024
 FIRST_X_COLS = 2 * P
@@ -31,8 +32,8 @@ FIRST_X_COLS = 2 * P
 
 def regroup(copy, grouped, planes):
     copy(
-        out=grouped.rearrange("p (c r) t -> p c t r", r=4),
-        in_=planes.rearrange("p t (c r) -> p c t r", r=4),
+        out=grouped.rearrange("p (c r) t -> p c t r", r=RUN),
+        in_=planes.rearrange("p t (c r) -> p c t r", r=RUN),
     )
 
 

@@ -23,7 +23,7 @@ HALF = D // 2
 GPSIMD_EARLY = 4
 LATE_OUTPUT_FROM = MODELS - 2
 SCALAR_REGROUPS_G_FROM = MODELS - 1
-E_EARLY = 2 * MODELS - 3
+E_EARLY = 2 * MODELS - 2
 RUN = 8
 HOLD_COLS = 8
 X_HALF = 1024
@@ -85,12 +85,12 @@ def tile_model_pa_kernel(tc, x, emb_W, emb_b, enc_W1, enc_b1, enc_W2, enc_b2, ou
         x_v = x.rearrange("b c (l y) -> (b c) l y", l=2)
         nc.scalar.dma_start(out=eb_bf[:], in_=emb_b.rearrange("(p t) -> p t", t=PACK))
         nc.scalar.dma_start(out=brows[0:MODELS, :], in_=enc_b1)
-        nc.sync.dma_start(out=embw[:], in_=emb_W)
         nc.sync.dma_start(out=x_sb[:, :, 0:FIRST_X_COLS], in_=x_v[:, :, 0:FIRST_X_COLS])
+        nc.sync.dma_start(out=embw[:], in_=emb_W)
         nc.sync.dma_start(out=x_sb[:, :, FIRST_X_COLS:X_HALF // 2], in_=x_v[:, :, FIRST_X_COLS:X_HALF // 2])
         load_weights(0)
         nc.sync.dma_start(out=x_sb[:, :, X_HALF // 2:X_HALF], in_=x_v[:, :, X_HALF // 2:X_HALF])
-        for i in (2, 4, 1, 6):
+        for i in (2, 4, 6, 1):
             load_weights(i)
         for n in range(1, MODELS):
             load_weights(2 * n + 1)
@@ -283,14 +283,14 @@ def tile_model_pa_kernel(tc, x, emb_W, emb_b, enc_W1, enc_b1, enc_W2, enc_b2, ou
             w_tile(i)
         nc.vector.tensor_copy(out=embwp[:], in_=embw[:].rearrange("p (m t) -> p t m", t=PACK))
         nc.vector.tensor_copy(out=eb[:], in_=eb_bf[:])
-        x_transpose(0, 1, "a0", nc.vector.tensor_copy)
+        x_transpose(0, 1, "a0", nc.scalar.copy)
         x_transpose(1, 1, "a1", nc.scalar.copy)
         for half in range(4):
             embed(half, e_bank(half))
         x_transpose(2, 2, "a2", nc.scalar.copy)
-        for i in (0, 2, 4, 1, 6):
+        for i in (0, 2, 4, 6):
             gpsimd_copy(wg[i][:, HALF:D, :], i, HALF, D)
-        early = (0, 2, 4, 1, 6)
+        early = (0, 2, 4, 6, 1)
         for n in range(MODELS):
             for half in (2 * n, 2 * n + 1):
                 if half < E_EARLY:
@@ -311,6 +311,7 @@ def tile_model_pa_kernel(tc, x, emb_W, emb_b, enc_W1, enc_b1, enc_W2, enc_b2, ou
             e_quantise(n)
             layer1(n)
         w_quantise(4)
+        regroup(nc.vector.tensor_copy, wg[1][:, HALF:D, :], wraw[1][:, :, HALF:D])
         w_regroup_tensor(2 * GPSIMD_EARLY)
         w_tile(3)
         w_regroup_scalar(3, 0, HALF)
@@ -341,10 +342,10 @@ def tile_model_pa_kernel(tc, x, emb_W, emb_b, enc_W1, enc_b1, enc_W2, enc_b2, ou
                 w_quantise_scalar_half(2 * step + 1)
             else:
                 w_quantise(2 * step + 1)
-            if step + 1 in (MODELS - 2, MODELS - 1):
-                w_quantise_gpsimd(2 * (step + 1) + 1)
             g_quantise(step)
             layer2(step)
+            if step + 1 in (MODELS - 2, MODELS - 1):
+                w_quantise_gpsimd(2 * (step + 1) + 1)
             if is_model(step + 5):
                 w_regroup_tensor(2 * (step + 5))
             if step + 3 < GPSIMD_EARLY:

from contextlib import ExitStack

import concourse.mybir as mybir
from concourse.masks import make_identity

BF16 = mybir.dt.bfloat16
F32 = mybir.dt.float32
U32 = mybir.dt.uint32
U8 = mybir.dt.uint8
FP8X4 = mybir.dt.float8_e4m3fn_x4
ADD = mybir.AluOpType.add
MULT = mybir.AluOpType.mult
GELU = mybir.ActivationFunctionType.Gelu_apprx_tanh

P = 128
PACK = 4
MODELS = 8
D = 512
TOKENS = 256
FLOPS = 2 * 2048 * 128 * 512 + 2 * 2 * 2048 * 512 * 512

HALF = D // 2
GPSIMD_EARLY = 4
LATE_OUTPUT_FROM = MODELS - 2
SCALAR_REGROUPS_G_FROM = MODELS - 1
E_EARLY = 2 * MODELS - 2
RUN = 8
HOLD_COLS = 8
X_HALF = 1024
FIRST_X_COLS = 2 * P


def regroup(copy, grouped, planes):
    copy(
        out=grouped.rearrange("p (c r) t -> p c t r", r=RUN),
        in_=planes.rearrange("p t (c r) -> p c t r", r=RUN),
    )


def tile_model_pa_kernel(tc, x, emb_W, emb_b, enc_W1, enc_b1, enc_W2, enc_b2, out):
    nc = tc.nc
    with ExitStack() as ctx:
        const = ctx.enter_context(tc.tile_pool(name="const", bufs=1))
        wraw_pool = ctx.enter_context(tc.tile_pool(name="wraw", bufs=1))
        wq_pool = ctx.enter_context(tc.tile_pool(name="wq", bufs=1))
        grp = ctx.enter_context(tc.tile_pool(name="grp", bufs=8))
        act = ctx.enter_context(tc.tile_pool(name="act", bufs=3))
        psum = ctx.enter_context(tc.psum_pool(name="psum", bufs=1))
        ctx.enter_context(tc.manual_schedule())

        def is_model(n):
            return 0 <= n < MODELS

        wraw = []
        wc = []
        ws = []
        for i in range(2 * MODELS):
            wraw.append(wraw_pool.tile([P, PACK, D], BF16, name="wraw%d" % i))
            wc.append(wq_pool.tile([P, D], U32, name="wc%d" % i, align_bytes=64))
            ws.append(wq_pool.tile([P, D], U8, name="ws%d" % i, align_bytes=64))
        x_sb = const.tile([P, 2, X_HALF], BF16, name="x_sb")
        embw = const.tile([P, D], BF16, name="embw")
        embwp = const.tile([P, PACK, P], BF16, name="embwp")
        eb_bf = const.tile([P, PACK], BF16, name="eb_bf")
        eb = const.tile([P, PACK], F32, name="eb")
        brows = const.tile([P, D], BF16, name="brows")
        b1T = const.tile([P, PACK, MODELS], F32, name="b1T")
        b2bc = const.tile([P, MODELS, D], BF16, name="b2bc")
        warm = const.tile([P, 1], F32, name="warm")
        warm2 = const.tile([P, 1], F32, name="warm2")
        ident = const.tile([P, P], BF16, name="ident")
        xT = const.tile([P, MODELS, 2, P], BF16, name="xT")

        def load_weights(i):
            n = i // 2
            if i % 2 == 0:
                src = enc_W1[n].rearrange("(p t) h -> p t h", t=PACK)
            else:
                src = enc_W2[n].rearrange("(t p) d -> p t d", p=P)
            nc.sync.dma_start(out=wraw[i][:], in_=src)

        nc.vector.memset(brows[:], 0.0)
        nc.vector.memset(warm[:], 0.0)
        make_identity(nc, ident[:])
        x_v = x.rearrange("b c (l y) -> (b c) l y", l=2)
        nc.scalar.dma_start(out=eb_bf[:], in_=emb_b.rearrange("(p t) -> p t", t=PACK))
        nc.scalar.dma_start(out=brows[0:MODELS, :], in_=enc_b1)
        nc.sync.dma_start(out=x_sb[:, :, 0:FIRST_X_COLS], in_=x_v[:, :, 0:FIRST_X_COLS])
        nc.sync.dma_start(out=embw[:], in_=emb_W)
        nc.sync.dma_start(out=x_sb[:, :, FIRST_X_COLS:X_HALF // 2], in_=x_v[:, :, FIRST_X_COLS:X_HALF // 2])
        load_weights(0)
        nc.sync.dma_start(out=x_sb[:, :, X_HALF // 2:X_HALF], in_=x_v[:, :, X_HALF // 2:X_HALF])
        for i in (2, 4, 6, 1):
            load_weights(i)
        for n in range(1, MODELS):
            load_weights(2 * n + 1)
            if is_model(n + 3):
                load_weights(2 * (n + 3))
            if n % 2 == 1:
                nc.sync.dma_start(
                    out=b2bc[:, n - 1:n + 1, :].rearrange("p n d -> p (n d)"),
                    in_=enc_b2[n - 1:n + 1, :].rearrange("n d -> (n d)").partition_broadcast(P),
                )
        nc.scalar.activation(out=warm2[:], in_=warm[:], func=GELU)

        wg = {}
        wgg = {}

        def w_tile(i):
            wg[i] = grp.tile([P, D, PACK], BF16, name="wg", tag="wg", align_bytes=64)

        def w_regroup_scalar(i, c0, c1):
            regroup(nc.scalar.copy, wg[i][:, c0:c1, :], wraw[i][:, :, c0:c1])

        w_ps = {}

        def w_regroup_tensor(i):
            w_ps[i] = psum.tile([P, HALF, PACK], BF16, name="w_ps", tag="e1")
            for c0 in range(0, HALF, P):
                nc.tensor.matmul(
                    w_ps[i][:, c0:c0 + P, :].rearrange("p c t -> p (c t)"),
                    lhsT=ident[:],
                    rhs=wraw[i][:, :, c0:c0 + P].rearrange("p t c -> p c t"),
                    start=True,
                    stop=True,
                )

        def w_out_of_psum(i):
            nc.scalar.copy(
                out=wg[i][:, 0:HALF, :].rearrange("p c t -> p (c t)"), in_=w_ps[i][:].rearrange("p c t -> p (c t)")
            )

        def gpsimd_copy(dst, i, c0, c1):
            nc.gpsimd.tensor_scalar(
                out=dst,
                in0=wraw[i][:, :, c0:c1].rearrange("p t c -> p c t"),
                scalar1=1.0,
                scalar2=0.0,
                op0=MULT,
                op1=ADD,
            )

        def quantise_cols(i, grouped, c0, width):
            nc.vector.quantize_mx(
                out=wc[i][:, c0:c0 + width].bitcast(FP8X4),
                scales=ws[i][:, c0:c0 + width],
                in_=grouped.rearrange("p c t -> p (c t)"),
            )

        def w_quantise(i):
            quantise_cols(i, wg[i][:], 0, D)

        def w_quantise_scalar_half(i):
            quantise_cols(i, wg[i][:, 0:HALF, :], 0, HALF)

        def w_hold_gpsimd(i):
            wgg[i] = grp.tile([P, HALF, PACK], BF16, name="wgg", tag="wgg", bufs=1, align_bytes=64)
            nc.vector.memset(wgg[i][:, 0:HOLD_COLS, :], 0.0)

        def w_regroup_gpsimd(i):
            if i not in wgg:
                wgg[i] = grp.tile([P, HALF, PACK], BF16, name="wgg", tag="wgg", bufs=1, align_bytes=64)
            gpsimd_copy(wgg[i][:], i, HALF, D)

        def w_quantise_gpsimd(i):
            quantise_cols(i, wgg[i][:], HALF, HALF)

        def x_transpose(n0, count, bank, copy):
            x_ps = psum.tile([P, 2 * count, P], BF16, name="x_ps", tag=bank)
            for nn in range(count):
                for l in range(2):
                    c0 = (n0 + nn) * P
                    nc.tensor.transpose(x_ps[:, 2 * nn + l, :], x_sb[:, l, c0:c0 + P], ident[:])
            copy(out=xT[:, n0:n0 + count, :, :].rearrange("p n l c -> p (n l) c"), in_=x_ps[:])

        e_ps = {}
        ge = {}
        ec = {}
        es = {}
        a_ps = {}
        gT = {}
        gg = {}
        gc = {}
        gs = {}
        o_ps = {}

        def embed(half, bank):
            e_ps[half] = psum.tile([P, PACK, P], F32, name="e_ps", tag=bank)
            for t in range(PACK):
                nc.tensor.matmul(
                    e_ps[half][:, t, :], lhsT=embwp[:, t, :], rhs=xT[:, half // 2, half % 2, :], start=True, stop=True
                )

        def e_out_of_psum(half):
            n, l = divmod(half, 2)
            if l == 0:
                ge[n] = act.tile([P, TOKENS, PACK], BF16, name="ge", tag="ge", bufs=MODELS, align_bytes=64)
            nc.vector.tensor_tensor(
                out=ge[n][:, l * P:(l + 1) * P, :],
                in0=e_ps[half][:].rearrange("p t c -> p c t"),
                in1=eb[:].unsqueeze(1).to_broadcast([P, P, PACK]),
                op=ADD,
            )

        def e_quantise(n):
            ec[n] = act.tile([P, TOKENS], U32, name="ec", tag="ec", align_bytes=64)
            es[n] = act.tile([P, TOKENS], U8, name="es", tag="es", align_bytes=64)
            nc.vector.quantize_mx(
                out=ec[n][:].bitcast(FP8X4),
                scales=es[n][:],
                in_=ge[n][:].rearrange("p c t -> p (c t)"),
            )

        def e_bank(half):
            return ("e0", "e1", "o0", "o1")[half % 4]

        def layer1(n):
            for t_hi in range(2):
                a = psum.tile([P, 2, TOKENS], F32, name="a_ps", tag="a%d" % ((2 * n + t_hi) % 4))
                a_ps[(n, t_hi)] = a
                for t_lo in range(2):
                    t = 2 * t_hi + t_lo
                    nc.tensor.matmul_mx(
                        out=a[:, t_lo, :],
                        lhsT=wc[2 * n][:, t * P:(t + 1) * P].bitcast(FP8X4),
                        lhsT_scale=ws[2 * n][:, t * P:(t + 1) * P],
                        rhs=ec[n][:].bitcast(FP8X4),
                        rhs_scale=es[n][:],
                        start=True,
                        stop=True,
                    )

        def gelu(n):
            gT[n] = act.tile([P, PACK, TOKENS], BF16, name="gT", tag="gT")
            for t in range(PACK):
                nc.scalar.activation(
                    out=gT[n][:, t, :], in_=a_ps[(n, t // 2)][:, t % 2, :], func=GELU, bias=b1T[:, t, n:n + 1]
                )

        def g_regroup(n, copy):
            gg[n] = act.tile([P, TOKENS, PACK], BF16, name="gg", tag="gg", align_bytes=64)
            regroup(copy, gg[n][:], gT[n][:])

        def g_quantise(n):
            gc[n] = act.tile([P, TOKENS], U32, name="gc", tag="gc", align_bytes=64)
            gs[n] = act.tile([P, TOKENS], U8, name="gs", tag="gs", align_bytes=64)
            nc.vector.quantize_mx(
                out=gc[n][:].bitcast(FP8X4),
                scales=gs[n][:],
                in_=gg[n][:].rearrange("p c t -> p (c t)"),
            )

        def layer2(n):
            for l in range(2):
                o = psum.tile([P, D], F32, name="o_ps", tag="%s%d" % ("e" if n == MODELS - 1 else "o", l))
                o_ps[(n, l)] = o
                nc.tensor.matmul_mx(
                    out=o[:],
                    lhsT=gc[n][:, l * P:(l + 1) * P].bitcast(FP8X4),
                    lhsT_scale=gs[n][:, l * P:(l + 1) * P],
                    rhs=wc[2 * n + 1][:].bitcast(FP8X4),
                    rhs_scale=ws[2 * n + 1][:],
                    start=True,
                    stop=True,
                )

        def output(n, store_each_piece):
            o_sb = act.tile([P, 2, D], F32, name="o_sb", tag="o_sb", bufs=8)
            dst = out[n].rearrange("b c l d -> (b c) l d")
            for l in range(2):
                width = HALF if (store_each_piece and l == 1) else D
                for d0 in range(0, D, width):
                    cols = slice(d0, d0 + width)
                    nc.vector.tensor_tensor(
                        out=o_sb[:, l, cols], in0=o_ps[(n, l)][:, cols], in1=b2bc[:, n, cols], op=ADD
                    )
                    if store_each_piece:
                        nc.sync.dma_start(out=dst[:, l, cols], in_=o_sb[:, l, cols])
            if not store_each_piece:
                nc.sync.dma_start(out=dst, in_=o_sb[:])

        for i in (0, 2, 4, 1, 6):
            w_tile(i)
        nc.vector.tensor_copy(out=embwp[:], in_=embw[:].rearrange("p (m t) -> p t m", t=PACK))
        nc.vector.tensor_copy(out=eb[:], in_=eb_bf[:])
        x_transpose(0, 1, "a0", nc.scalar.copy)
        x_transpose(1, 1, "a1", nc.scalar.copy)
        for half in range(4):
            embed(half, e_bank(half))
        x_transpose(2, 2, "a2", nc.scalar.copy)
        for i in (0, 2, 4, 6):
            gpsimd_copy(wg[i][:, HALF:D, :], i, HALF, D)
        early = (0, 2, 4, 6, 1)
        for n in range(MODELS):
            for half in (2 * n, 2 * n + 1):
                if half < E_EARLY:
                    e_out_of_psum(half)
            for half in (2 * n + 4, 2 * n + 5):
                if half < E_EARLY:
                    embed(half, e_bank(half))
            if n < len(early):
                w_regroup_scalar(early[n], 0, HALF)
            if n < 2:
                x_transpose(4 + 2 * n, 2, "a%d" % (3 * (1 - n)), nc.scalar.copy)
        bt_ps = psum.tile([P, PACK, P], BF16, name="bt_ps", tag="a0")
        for t in range(PACK):
            nc.tensor.transpose(bt_ps[:, t, :], brows[:, t * P:(t + 1) * P], ident[:])
        nc.vector.tensor_copy(out=b1T[:], in_=bt_ps[:, :, 0:MODELS])
        for n in range(2):
            w_quantise(2 * n)
            e_quantise(n)
            layer1(n)
        w_quantise(4)
        regroup(nc.vector.tensor_copy, wg[1][:, HALF:D, :], wraw[1][:, :, HALF:D])
        w_regroup_tensor(2 * GPSIMD_EARLY)
        w_tile(3)
        w_regroup_scalar(3, 0, HALF)
        gelu(0)
        w_regroup_scalar(3, HALF, D)

        for step in range(MODELS):
            if is_model(step + 1):
                gelu(step + 1)
                if step + 1 >= SCALAR_REGROUPS_G_FROM:
                    g_regroup(step + 1, nc.scalar.copy)
            if is_model(step + 4):
                w_tile(2 * (step + 4))
                w_out_of_psum(2 * (step + 4))
            if is_model(step + 2):
                i = 2 * (step + 2) + 1
                w_tile(i)
                w_regroup_scalar(i, 0, HALF if step + 2 >= MODELS - 2 else D)
            late_half = E_EARLY + step - 1
            if E_EARLY <= late_half < 2 * MODELS:
                embed(late_half, "e0")
            if is_model(step + 2):
                e_quantise(step + 2)
                layer1(step + 2)
            if step < SCALAR_REGROUPS_G_FROM:
                g_regroup(step, nc.vector.tensor_copy)
            if step >= MODELS - 2:
                w_quantise_scalar_half(2 * step + 1)
            else:
                w_quantise(2 * step + 1)
            g_quantise(step)
            layer2(step)
            if step + 1 in (MODELS - 2, MODELS - 1):
                w_quantise_gpsimd(2 * (step + 1) + 1)
            if is_model(step + 5):
                w_regroup_tensor(2 * (step + 5))
            if step + 3 < GPSIMD_EARLY:
                w_hold_gpsimd(2 * (step + 4))
                w_quantise(2 * (step + 3))
            elif is_model(step + 3):
                w_quantise_gpsimd(2 * (step + 3))
                w_quantise_scalar_half(2 * (step + 3))
            if is_model(step + 4):
                w_regroup_gpsimd(2 * (step + 4))
            elif step + 2 in (MODELS - 2, MODELS - 1):
                w_regroup_gpsimd(2 * (step + 2) + 1)
            if E_EARLY <= late_half < 2 * MODELS:
                e_out_of_psum(late_half)
            if step < LATE_OUTPUT_FROM:
                output(step, False)
            if step > LATE_OUTPUT_FROM:
                output(step - 1, False)
            if step == MODELS - 1:
                output(step, True)
